import numpy as np
import ml_dtypes


def mxq(x, axis, fmt="e4m3"):
    dtype, down = {"e4m3": (ml_dtypes.float8_e4m3fn, 7), "e5m2": (ml_dtypes.float8_e5m2, 14)}[fmt]
    v = np.moveaxis(np.asarray(x, np.float32).astype(ml_dtypes.bfloat16).astype(np.float64), axis, -1)
    blocks = v.reshape(v.shape[:-1] + (-1, 32))
    amax = np.abs(blocks).max(-1, keepdims=True)
    byte = np.maximum(np.where(amax > 0, np.frexp(amax)[1] - 1 + 127, 0) - down, 1)
    scale = np.exp2(byte - 127.0)
    codes = (blocks / scale).astype(np.float32).astype(dtype).astype(np.float64)
    return np.moveaxis((codes * scale).reshape(v.shape), -1, axis)


WIDE = False


def mx_kscale(k):
    if not WIDE:
        return np.ones(k)
    levels = np.array([10, -10, 5, -5, 0])
    a = np.random.permutation(np.resize(levels, k // 512 * 4)).reshape(k // 512, 4)
    idx = np.arange(k)
    return np.exp2(a[idx // 512, idx % 128 // 32])


BF16 = ml_dtypes.bfloat16


def bf(x):
    return np.asarray(x, np.float32).astype(BF16)


def f64(x):
    return np.asarray(x).astype(np.float64)


B, S, DIM, QL, KVL, H, DN, DR, DV, P0 = 2, 256, 2048, 1536, 512, 16, 128, 128, 128, 37
EPS = 1e-6
HALF = DR // 2


def rms_norm(v, w):
    return v / np.sqrt(np.mean(v * v, axis=-1, keepdims=True) + EPS) * w


def rope(v, start):
    theta = 10000.0 ** (-np.arange(HALF) / HALF)
    pos = np.arange(v.shape[-2]) + start
    ang = pos[:, None] * theta[None, :]
    ang2 = np.concatenate([ang, ang], axis=-1)
    v1, v2 = v[..., :HALF], v[..., HALF:]
    rot = np.concatenate([-v2, v1], axis=-1)
    return v * np.cos(ang2) + rot * np.sin(ang2)


def setup_inputs():
    s = mx_kscale(DIM)
    return {"x": bf(np.random.standard_normal((B, S, DIM)) * s),
            "wkv_a": bf(np.random.standard_normal((DIM, KVL + DR)) / np.sqrt(DIM) / s[:, None]),
            "wkv_b": bf(np.random.standard_normal((KVL, H * (DN + DV))) / np.sqrt(KVL))}


def reference(x, wkv_a, wkv_b):
    kv = mxq(f64(x), 2, "e4m3") @ mxq(f64(wkv_a), 0, "e4m3")
    kv_c, k_pe = kv[..., :KVL], kv[..., KVL:]
    k_pe = rope(k_pe[:, :, None, :], P0)
    cn = rms_norm(kv_c, np.ones(KVL))
    kv_up = (mxq(cn, 2, "e4m3") @ mxq(f64(wkv_b), 0, "e4m3")).reshape(B, S, H, DN + DV)
    k_nope, v = kv_up[..., :DN], kv_up[..., DN:]
    k = np.concatenate([k_nope, np.broadcast_to(k_pe, (B, S, H, DR))], axis=-1)
    return k, v

@@ -1,0 +1,344 @@
+import math
+from contextlib import ExitStack
+
+import concourse.mybir as mybir
+from concourse.masks import make_identity
+
+F32 = mybir.dt.float32
+BF16 = mybir.dt.bfloat16
+I32 = mybir.dt.int32
+U32 = mybir.dt.uint32
+U8 = mybir.dt.uint8
+FP8X4 = mybir.dt.float8_e4m3fn_x4
+ALU = mybir.AluOpType
+ACT = mybir.ActivationFunctionType
+
+P = 128
+PACK = 4
+K_PASS = P * PACK
+PSUM_BANKS = 8
+
+TOKENS = 512
+TOKEN_TILES = TOKENS // P
+DIM = 2048
+A_PASSES = DIM // K_PASS
+LATENT = 512
+ROPE_DIM = 128
+HALF = ROPE_DIM // 2
+DOUBLINGS = 6
+assert 2**DOUBLINGS == HALF
+A_COLS = LATENT + ROPE_DIM
+HEADS = 16
+HEAD_DIM = 128
+EPS = 1e-6
+ROPE_BASE = 10000.0
+POSITION = 37
+
+PIECE_HEADS = 4
+PIECES = HEADS // PIECE_HEADS
+PIECE_COLS = PIECE_HEADS * 2 * HEAD_DIM
+B_UNIT_COLS = 512
+A_VECTOR_COLS = A_COLS // 2
+RUN = 4
+OUT_BUFS = 8
+
+FLOPS = 2 * TOKENS * DIM * A_COLS + 2 * TOKENS * LATENT * HEADS * 2 * HEAD_DIM
+
+
+def regroup(copy, grouped, raw):
+    copy(
+        out=grouped.rearrange("p (c i) t -> p c t i", i=RUN),
+        in_=raw.rearrange("p t (c i) -> p c t i", i=RUN),
+    )
+
+
+def build_rope_table(nc, pool):
+    theta = pool.tile([P, HALF], F32, name="theta")
+    nc.vector.memset(theta[:, 0:1], 1.0)
+    for step in range(DOUBLINGS):
+        width = 2**step
+        nc.vector.tensor_scalar(
+            out=theta[:, width : 2 * width],
+            in0=theta[:, 0:width],
+            scalar1=ROPE_BASE ** (-width / HALF),
+            scalar2=None,
+            op0=ALU.mult,
+        )
+    turns = pool.tile([P, 2, HALF], F32, name="turns")
+    per_turn = POSITION / (2.0 * math.pi)
+    nc.vector.tensor_scalar(
+        out=turns[:, 0, :], in0=theta[:], scalar1=per_turn, scalar2=0.25, op0=ALU.mult, op1=ALU.add
+    )
+    nc.vector.tensor_scalar(
+        out=turns[:, 1, :], in0=theta[:], scalar1=per_turn, scalar2=None, op0=ALU.mult
+    )
+    whole_int = pool.tile([P, 2, HALF], I32, name="whole_int")
+    nc.vector.tensor_copy(out=whole_int[:], in_=turns[:])
+    whole = pool.tile([P, 2, HALF], F32, name="whole")
+    nc.vector.tensor_copy(out=whole[:], in_=whole_int[:])
+    left = pool.tile([P, 2, HALF], F32, name="left")
+    nc.vector.tensor_tensor(out=left[:], in0=turns[:], in1=whole[:], op=ALU.subtract)
+    minus = pool.tile([P, 2, HALF], F32, name="minus")
+    nc.vector.scalar_tensor_tensor(
+        out=minus[:], in0=left[:], scalar=0.5, in1=left[:], op0=ALU.is_gt, op1=ALU.subtract
+    )
+    trig = pool.tile([P, 2, HALF], F32, name="trig")
+    nc.scalar.activation(out=trig[:], in_=minus[:], func=ACT.Sin, scale=-2.0 * math.pi)
+    return trig
+
+
+def tile_mla_pb_kernel(tc, x, wkv_a, wkv_b, out_0, out_1):
+    nc = tc.nc
+    x_rows = x.rearrange("b s d -> (b s) d")
+    k_rows = out_0.rearrange("b s h d -> (b s) h d")
+    v_rows = out_1.rearrange("b s h d -> (b s) h d")
+
+    with ExitStack() as stack:
+        stack.enter_context(tc.manual_schedule())
+        keep = stack.enter_context(tc.tile_pool(name="keep", bufs=1))
+        stage = stack.enter_context(tc.tile_pool(name="stage", bufs=2))
+        b_stage = stack.enter_context(tc.tile_pool(name="b_stage", bufs=4))
+        outs = stack.enter_context(tc.tile_pool(name="outs", bufs=OUT_BUFS))
+        psum = stack.enter_context(tc.psum_pool(name="psum", bufs=PSUM_BANKS))
+
+        x_raw = []
+        for i in range(TOKEN_TILES):
+            raw = keep.tile([P, DIM], BF16, name="x_raw%d" % i)
+            nc.sync.dma_start(out=raw[:], in_=x_rows[i * P : (i + 1) * P, :])
+            x_raw.append(raw)
+        a_raw = []
+        for g in range(A_PASSES):
+            raw = keep.tile([P, PACK, A_COLS], BF16, name="a_raw%d" % g)
+            rows = wkv_a[g * K_PASS : (g + 1) * K_PASS, :]
+            nc.sync.dma_start(out=raw[:], in_=rows.rearrange("(p t) c -> p t c", t=PACK))
+            a_raw.append(raw)
+        b_raw = []
+        for piece in range(PIECES):
+            raw = keep.tile([P, PACK, PIECE_COLS], BF16, name="b_raw%d" % piece)
+            cols = wkv_b[:, piece * PIECE_COLS : (piece + 1) * PIECE_COLS]
+            nc.sync.dma_start(out=raw[:], in_=cols.rearrange("(p t) c -> p t c", t=PACK))
+            b_raw.append(raw)
+
+        ident_f32 = keep.tile([P, P], F32, name="ident_f32")
+        make_identity(nc, ident_f32[:])
+        ident_bf16 = keep.tile([P, P], BF16, name="ident_bf16")
+        make_identity(nc, ident_bf16[:])
+        eps = keep.tile([P, 1], F32, name="eps")
+        nc.vector.memset(eps[:], EPS)
+        trig = build_rope_table(nc, keep)
+        warm_up = keep.tile([P, 1], F32, name="warm_up")
+        nc.scalar.activation(out=warm_up[:], in_=eps[:], func=ACT.Abs_reciprocal_sqrt)
+
+        x_codes = keep.tile([P, TOKEN_TILES, A_PASSES, P], U32, name="x_codes", align_bytes=64)
+        x_scales = keep.tile([P, TOKEN_TILES, A_PASSES, P], U8, name="x_scales", align_bytes=64)
+        a_codes = keep.tile([P, A_PASSES, A_COLS], U32, name="a_codes", align_bytes=64)
+        a_scales = keep.tile([P, A_PASSES, A_COLS], U8, name="a_scales", align_bytes=64)
+        cn_codes = keep.tile([P, TOKEN_TILES, P], U32, name="cn_codes", align_bytes=64)
+        cn_scales = keep.tile([P, TOKEN_TILES, P], U8, name="cn_scales", align_bytes=64)
+        b_codes = keep.tile([P, HEADS, 2, HEAD_DIM], U32, name="b_codes", align_bytes=64)
+        b_scales = keep.tile([P, HEADS, 2, HEAD_DIM], U8, name="b_scales", align_bytes=64)
+
+        for i in range(TOKEN_TILES):
+            words = x_raw[i][:].bitcast(F32).rearrange("p (g q u) -> p g u q", g=A_PASSES, u=2)
+            x_grouped = stage.tile([P, A_PASSES * P * PACK], BF16, name="x_grouped", align_bytes=64)
+            grouped_words = x_grouped[:].bitcast(F32).rearrange(
+                "p (g w u) -> p g w u", g=A_PASSES, u=2
+            )
+            for bank_no, copy in enumerate((nc.scalar.copy, nc.vector.tensor_copy)):
+                x_bank = psum.tile([P, 2, 2, P], F32, name="x_bank", tag="bank")
+                for g in range(2):
+                    for u in range(2):
+                        nc.tensor.transpose(
+                            x_bank[:, g, u, :], words[:, 2 * bank_no + g, u, :], ident_f32[:]
+                        )
+                copy(
+                    out=grouped_words[:, 2 * bank_no : 2 * bank_no + 2, :, :],
+                    in_=x_bank[:].rearrange("p g u w -> p g w u"),
+                )
+            nc.vector.quantize_mx(
+                out=x_codes[:, i, :, :].rearrange("p g w -> p (g w)").bitcast(FP8X4),
+                scales=x_scales[:, i, :, :].rearrange("p g w -> p (g w)"),
+                in_=x_grouped[:],
+            )
+
+        c_banks = []
+        for i in range(TOKEN_TILES):
+            c_bank = psum.tile([P, LATENT], F32, name="c_bank%d" % i, tag="bank")
+            c_banks.append(c_bank)
+        for g in range(A_PASSES):
+            a_grouped = stage.tile([P, A_COLS, PACK], BF16, name="a_grouped", align_bytes=64)
+            regroup(
+                nc.vector.tensor_copy,
+                a_grouped[:, 0:A_VECTOR_COLS, :],
+                a_raw[g][:, :, 0:A_VECTOR_COLS],
+            )
+            regroup(
+                nc.scalar.copy,
+                a_grouped[:, A_VECTOR_COLS:A_COLS, :],
+                a_raw[g][:, :, A_VECTOR_COLS:A_COLS],
+            )
+            for first, last in ((0, LATENT), (LATENT, A_COLS)):
+                nc.vector.quantize_mx(
+                    out=a_codes[:, g, first:last].bitcast(FP8X4),
+                    scales=a_scales[:, g, first:last],
+                    in_=a_grouped[:, first:last, :].rearrange("p c t -> p (c t)"),
+                )
+            for i in range(TOKEN_TILES):
+                nc.tensor.matmul_mx(
+                    out=c_banks[i][:],
+                    lhsT=x_codes[:, i, g, :].bitcast(FP8X4),
+                    lhsT_scale=x_scales[:, i, g, :],
+                    rhs=a_codes[:, g, 0:LATENT].bitcast(FP8X4),
+                    rhs_scale=a_scales[:, g, 0:LATENT],
+                    start=(g == 0),
+                    stop=(g == A_PASSES - 1),
+                )
+
+        r_bank = psum.tile([P, TOKEN_TILES, ROPE_DIM], F32, name="r_bank", tag="bank")
+        for i in range(TOKEN_TILES):
+            for g in range(A_PASSES):
+                nc.tensor.matmul_mx(
+                    out=r_bank[:, i, :],
+                    lhsT=x_codes[:, i, g, :].bitcast(FP8X4),
+                    lhsT_scale=x_scales[:, i, g, :],
+                    rhs=a_codes[:, g, LATENT:A_COLS].bitcast(FP8X4),
+                    rhs_scale=a_scales[:, g, LATENT:A_COLS],
+                    start=(g == 0),
+                    stop=(g == A_PASSES - 1),
+                )
+
+        def quantise_b(piece):
+            units = PIECE_COLS // B_UNIT_COLS
+            heads_of_unit = B_UNIT_COLS // (2 * HEAD_DIM)
+            grouped_units = []
+            for unit in range(units):
+                b_grouped = b_stage.tile(
+                    [P, B_UNIT_COLS, PACK], BF16, name="b_grouped", align_bytes=64
+                )
+                regroup(
+                    nc.vector.tensor_copy,
+                    b_grouped[:],
+                    b_raw[piece][:, :, unit * B_UNIT_COLS : (unit + 1) * B_UNIT_COLS],
+                )
+                grouped_units.append(b_grouped)
+            for unit in range(units):
+                head = piece * PIECE_HEADS + unit * heads_of_unit
+                nc.vector.quantize_mx(
+                    out=b_codes[:, head : head + heads_of_unit, :, :]
+                    .rearrange("p h f d -> p (h f d)")
+                    .bitcast(FP8X4),
+                    scales=b_scales[:, head : head + heads_of_unit, :, :].rearrange(
+                        "p h f d -> p (h f d)"
+                    ),
+                    in_=grouped_units[unit][:].rearrange("p c t -> p (c t)"),
+                )
+
+        def rotate_rope_key():
+            halves = TOKEN_TILES * 2
+            products = keep.tile([P, 2, halves, HALF], F32, name="products")
+            nc.vector.tensor_tensor(
+                out=products[:],
+                in0=r_bank[:]
+                .rearrange("p i (h j) -> p (i h) j", j=HALF)
+                .unsqueeze(1)
+                .to_broadcast([P, 2, halves, HALF]),
+                in1=trig[:].unsqueeze(2).to_broadcast([P, 2, halves, HALF]),
+                op=ALU.mult,
+            )
+            by_half = products[:].rearrange("p f (i h) j -> p f i h j", h=2)
+            nc.vector.tensor_tensor(
+                out=rope[:, :, 0, :],
+                in0=by_half[:, 0, :, 0, :],
+                in1=by_half[:, 1, :, 1, :],
+                op=ALU.subtract,
+            )
+            nc.vector.tensor_tensor(
+                out=rope[:, :, 1, :],
+                in0=by_half[:, 0, :, 1, :],
+                in1=by_half[:, 1, :, 0, :],
+                op=ALU.add,
+            )
+
+        def norm_factor(i):
+            one = slice(i, i + 1)
+            squares = stage.tile([P, LATENT], F32, name="squares")
+            nc.scalar.activation(
+                out=squares[:], in_=c_banks[i][:], func=ACT.Square, accum_out=sum_squares[:, one]
+            )
+            nc.scalar.activation(
+                out=inv_rms[:, one],
+                in_=sum_squares[:, one],
+                func=ACT.Abs_reciprocal_sqrt,
+                scale=1.0 / LATENT,
+                bias=eps[:],
+            )
+
+        def quantise_cn(i):
+            cn = stage.tile([P, PACK, P], BF16, name="cn")
+            nc.scalar.activation(
+                out=cn[:],
+                in_=c_banks[i][:].rearrange("p (q t) -> p t q", t=PACK),
+                func=ACT.Copy,
+                scale=inv_rms[:, i : i + 1],
+            )
+            cn_bank = psum.tile([P, PACK, P], BF16, name="cn_bank", tag="bank")
+            for t in range(PACK):
+                nc.tensor.transpose(cn_bank[:, t, :], cn[:, t, :], ident_bf16[:])
+            cn_grouped = stage.tile([P, P, PACK], BF16, name="cn_grouped", align_bytes=64)
+            nc.vector.tensor_copy(out=cn_grouped[:], in_=cn_bank[:].rearrange("p t w -> p w t"))
+            nc.vector.quantize_mx(
+                out=cn_codes[:, i, :].bitcast(FP8X4),
+                scales=cn_scales[:, i, :],
+                in_=cn_grouped[:].rearrange("p w t -> p (w t)"),
+            )
+
+        def multiply_and_store(piece, i):
+            first_head = piece * PIECE_HEADS
+            nope_bank = psum.tile([P, PIECE_HEADS, HEAD_DIM], F32, name="nope_bank", tag="bank")
+            v_bank = psum.tile([P, PIECE_HEADS, HEAD_DIM], F32, name="v_bank", tag="bank")
+            for kind, bank in enumerate((nope_bank, v_bank)):
+                for h in range(PIECE_HEADS):
+                    nc.tensor.matmul_mx(
+                        out=bank[:, h, :],
+                        lhsT=cn_codes[:, i, :].bitcast(FP8X4),
+                        lhsT_scale=cn_scales[:, i, :],
+                        rhs=b_codes[:, first_head + h, kind, :].bitcast(FP8X4),
+                        rhs_scale=b_scales[:, first_head + h, kind, :],
+                        start=True,
+                        stop=True,
+                    )
+            k_out = outs.tile([P, PIECE_HEADS, HEAD_DIM + ROPE_DIM], F32, name="k_out")
+            v_out = outs.tile([P, PIECE_HEADS, HEAD_DIM], F32, name="v_out")
+            nc.vector.tensor_copy(
+                out=k_out[:, :, HEAD_DIM : HEAD_DIM + ROPE_DIM],
+                in_=rope[:, i, :, :]
+                .rearrange("p h j -> p (h j)")
+                .unsqueeze(1)
+                .to_broadcast([P, PIECE_HEADS, ROPE_DIM]),
+            )
+            nc.scalar.copy(out=k_out[:, :, 0:HEAD_DIM], in_=nope_bank[:])
+            nc.scalar.copy(out=v_out[:], in_=v_bank[:])
+            tokens = slice(i * P, (i + 1) * P)
+            heads = slice(first_head, first_head + PIECE_HEADS)
+            nc.sync.dma_start(out=k_rows[tokens, heads, :], in_=k_out[:])
+            nc.sync.dma_start(out=v_rows[tokens, heads, :], in_=v_out[:])
+
+        rope = keep.tile([P, TOKEN_TILES, 2, HALF], F32, name="rope")
+        sum_squares = keep.tile([P, TOKEN_TILES], F32, name="sum_squares")
+        inv_rms = keep.tile([P, TOKEN_TILES], F32, name="inv_rms")
+
+        quantise_b(0)
+        norm_factor(0)
+        norm_factor(1)
+        quantise_cn(0)
+        rotate_rope_key()
+        for i in range(TOKEN_TILES):
+            if i + 2 < TOKEN_TILES:
+                norm_factor(i + 2)
+            if i + 1 < TOKEN_TILES:
+                quantise_cn(i + 1)
+            multiply_and_store(0, i)
+        for piece in range(1, PIECES):
+            quantise_b(piece)
+            for i in range(TOKEN_TILES):
+                multiply_and_store(piece, i)

@@ -34,13 +34,17 @@ EPS = 1e-6
 ROPE_BASE = 10000.0
 POSITION = 37
 
-PIECE_HEADS = 4
-PIECES = HEADS // PIECE_HEADS
-PIECE_COLS = PIECE_HEADS * 2 * HEAD_DIM
-B_UNIT_COLS = 512
+CHUNK_HEADS = 4
+CHUNKS = HEADS // CHUNK_HEADS
+CHUNK_COLS = CHUNK_HEADS * 2 * HEAD_DIM
+NOPE = 0
+VALUE = 1
+STORE_HEADS = 2 * CHUNK_HEADS
+STORES = HEADS // STORE_HEADS
+CHUNKS_OF_STORE = STORE_HEADS // CHUNK_HEADS
 A_VECTOR_COLS = A_COLS // 2
 RUN = 4
-OUT_BUFS = 8
+V_BUFS = 4
 
 FLOPS = 2 * TOKENS * DIM * A_COLS + 2 * TOKENS * LATENT * HEADS * 2 * HEAD_DIM
 
@@ -98,7 +102,7 @@ def tile_mla_pb_kernel(tc, x, wkv_a, wkv_b, out_0, out_1):
         keep = stack.enter_context(tc.tile_pool(name="keep", bufs=1))
         stage = stack.enter_context(tc.tile_pool(name="stage", bufs=2))
         b_stage = stack.enter_context(tc.tile_pool(name="b_stage", bufs=4))
-        outs = stack.enter_context(tc.tile_pool(name="outs", bufs=OUT_BUFS))
+        outs = stack.enter_context(tc.tile_pool(name="outs", bufs=V_BUFS))
         psum = stack.enter_context(tc.psum_pool(name="psum", bufs=PSUM_BANKS))
 
         x_raw = []
@@ -113,10 +117,13 @@ def tile_mla_pb_kernel(tc, x, wkv_a, wkv_b, out_0, out_1):
             nc.sync.dma_start(out=raw[:], in_=rows.rearrange("(p t) c -> p t c", t=PACK))
             a_raw.append(raw)
         b_raw = []
-        for piece in range(PIECES):
-            raw = keep.tile([P, PACK, PIECE_COLS], BF16, name="b_raw%d" % piece)
-            cols = wkv_b[:, piece * PIECE_COLS : (piece + 1) * PIECE_COLS]
-            nc.sync.dma_start(out=raw[:], in_=cols.rearrange("(p t) c -> p t c", t=PACK))
+        for chunk in range(CHUNKS):
+            raw = keep.tile([P, PACK, CHUNK_HEADS, 2, HEAD_DIM], BF16, name="b_raw%d" % chunk)
+            cols = wkv_b[:, chunk * CHUNK_COLS : (chunk + 1) * CHUNK_COLS]
+            nc.sync.dma_start(
+                out=raw[:].rearrange("p t h f d -> p t (h f d)"),
+                in_=cols.rearrange("(p t) c -> p t c", t=PACK),
+            )
             b_raw.append(raw)
 
         ident_f32 = keep.tile([P, P], F32, name="ident_f32")
@@ -135,8 +142,8 @@ def tile_mla_pb_kernel(tc, x, wkv_a, wkv_b, out_0, out_1):
         a_scales = keep.tile([P, A_PASSES, A_COLS], U8, name="a_scales", align_bytes=64)
         cn_codes = keep.tile([P, TOKEN_TILES, P], U32, name="cn_codes", align_bytes=64)
         cn_scales = keep.tile([P, TOKEN_TILES, P], U8, name="cn_scales", align_bytes=64)
-        b_codes = keep.tile([P, HEADS, 2, HEAD_DIM], U32, name="b_codes", align_bytes=64)
-        b_scales = keep.tile([P, HEADS, 2, HEAD_DIM], U8, name="b_scales", align_bytes=64)
+        b_codes = keep.tile([P, 2, HEADS, HEAD_DIM], U32, name="b_codes", align_bytes=64)
+        b_scales = keep.tile([P, 2, HEADS, HEAD_DIM], U8, name="b_scales", align_bytes=64)
 
         for i in range(TOKEN_TILES):
             words = x_raw[i][:].bitcast(F32).rearrange("p (g q u) -> p g u q", g=A_PASSES, u=2)
@@ -207,31 +214,20 @@ def tile_mla_pb_kernel(tc, x, wkv_a, wkv_b, out_0, out_1):
                     stop=(g == A_PASSES - 1),
                 )
 
-        def quantise_b(piece):
-            units = PIECE_COLS // B_UNIT_COLS
-            heads_of_unit = B_UNIT_COLS // (2 * HEAD_DIM)
-            grouped_units = []
-            for unit in range(units):
-                b_grouped = b_stage.tile(
-                    [P, B_UNIT_COLS, PACK], BF16, name="b_grouped", align_bytes=64
-                )
-                regroup(
-                    nc.vector.tensor_copy,
-                    b_grouped[:],
-                    b_raw[piece][:, :, unit * B_UNIT_COLS : (unit + 1) * B_UNIT_COLS],
-                )
-                grouped_units.append(b_grouped)
-            for unit in range(units):
-                head = piece * PIECE_HEADS + unit * heads_of_unit
-                nc.vector.quantize_mx(
-                    out=b_codes[:, head : head + heads_of_unit, :, :]
-                    .rearrange("p h f d -> p (h f d)")
-                    .bitcast(FP8X4),
-                    scales=b_scales[:, head : head + heads_of_unit, :, :].rearrange(
-                        "p h f d -> p (h f d)"
-                    ),
-                    in_=grouped_units[unit][:].rearrange("p c t -> p (c t)"),
-                )
+        def quantise_b(chunk, kind):
+            b_grouped = b_stage.tile(
+                [P, CHUNK_HEADS * HEAD_DIM, PACK], BF16, name="b_grouped", align_bytes=64
+            )
+            nc.vector.tensor_copy(
+                out=b_grouped[:].rearrange("p (h c i) t -> p h c t i", h=CHUNK_HEADS, i=RUN),
+                in_=b_raw[chunk][:, :, :, kind, :].rearrange("p t h (c i) -> p h c t i", i=RUN),
+            )
+            heads = slice(chunk * CHUNK_HEADS, (chunk + 1) * CHUNK_HEADS)
+            nc.vector.quantize_mx(
+                out=b_codes[:, kind, heads, :].rearrange("p h d -> p (h d)").bitcast(FP8X4),
+                scales=b_scales[:, kind, heads, :].rearrange("p h d -> p (h d)"),
+                in_=b_grouped[:].rearrange("p c t -> p (c t)"),
+            )
 
         def rotate_rope_key():
             halves = TOKEN_TILES * 2
@@ -292,53 +288,69 @@ def tile_mla_pb_kernel(tc, x, wkv_a, wkv_b, out_0, out_1):
                 in_=cn_grouped[:].rearrange("p w t -> p (w t)"),
             )
 
-        def multiply_and_store(piece, i):
-            first_head = piece * PIECE_HEADS
-            nope_bank = psum.tile([P, PIECE_HEADS, HEAD_DIM], F32, name="nope_bank", tag="bank")
-            v_bank = psum.tile([P, PIECE_HEADS, HEAD_DIM], F32, name="v_bank", tag="bank")
-            for kind, bank in enumerate((nope_bank, v_bank)):
-                for h in range(PIECE_HEADS):
-                    nc.tensor.matmul_mx(
-                        out=bank[:, h, :],
-                        lhsT=cn_codes[:, i, :].bitcast(FP8X4),
-                        lhsT_scale=cn_scales[:, i, :],
-                        rhs=b_codes[:, first_head + h, kind, :].bitcast(FP8X4),
-                        rhs_scale=b_scales[:, first_head + h, kind, :],
-                        start=True,
-                        stop=True,
-                    )
-            k_out = outs.tile([P, PIECE_HEADS, HEAD_DIM + ROPE_DIM], F32, name="k_out")
-            v_out = outs.tile([P, PIECE_HEADS, HEAD_DIM], F32, name="v_out")
+        def repeat_rope_key(i):
             nc.vector.tensor_copy(
-                out=k_out[:, :, HEAD_DIM : HEAD_DIM + ROPE_DIM],
+                out=k_out[i][:, :, HEAD_DIM : HEAD_DIM + ROPE_DIM],
                 in_=rope[:, i, :, :]
                 .rearrange("p h j -> p (h j)")
                 .unsqueeze(1)
-                .to_broadcast([P, PIECE_HEADS, ROPE_DIM]),
+                .to_broadcast([P, STORE_HEADS, ROPE_DIM]),
             )
-            nc.scalar.copy(out=k_out[:, :, 0:HEAD_DIM], in_=nope_bank[:])
-            nc.scalar.copy(out=v_out[:], in_=v_bank[:])
-            tokens = slice(i * P, (i + 1) * P)
-            heads = slice(first_head, first_head + PIECE_HEADS)
-            nc.sync.dma_start(out=k_rows[tokens, heads, :], in_=k_out[:])
-            nc.sync.dma_start(out=v_rows[tokens, heads, :], in_=v_out[:])
+
+        def multiply_and_store(kind, store, i):
+            if kind == NOPE:
+                out_tile, out_rows, width = k_out[i], k_rows, HEAD_DIM + ROPE_DIM
+            else:
+                out_tile = outs.tile([P, STORE_HEADS, HEAD_DIM], F32, name="v_out")
+                out_rows, width = v_rows, HEAD_DIM
+            first_head = store * STORE_HEADS
+            for first in range(0, STORE_HEADS, CHUNK_HEADS):
+                u_bank = psum.tile([P, CHUNK_HEADS, HEAD_DIM], F32, name="u_bank", tag="bank")
+                for h in range(CHUNK_HEADS):
+                    nc.tensor.matmul_mx(
+                        out=u_bank[:, h, :],
+                        lhsT=cn_codes[:, i, :].bitcast(FP8X4),
+                        lhsT_scale=cn_scales[:, i, :],
+                        rhs=b_codes[:, kind, first_head + first + h, :].bitcast(FP8X4),
+                        rhs_scale=b_scales[:, kind, first_head + first + h, :],
+                        start=True,
+                        stop=True,
+                    )
+                nc.scalar.copy(
+                    out=out_tile[:, first : first + CHUNK_HEADS, 0:HEAD_DIM], in_=u_bank[:]
+                )
+            nc.sync.dma_start(
+                out=out_rows[i * P : (i + 1) * P, first_head : first_head + STORE_HEADS, :],
+                in_=out_tile[:, :, 0:width],
+            )
 
         rope = keep.tile([P, TOKEN_TILES, 2, HALF], F32, name="rope")
         sum_squares = keep.tile([P, TOKEN_TILES], F32, name="sum_squares")
         inv_rms = keep.tile([P, TOKEN_TILES], F32, name="inv_rms")
+        k_out = []
+        for i in range(TOKEN_TILES):
+            k_tile = keep.tile([P, STORE_HEADS, HEAD_DIM + ROPE_DIM], F32, name="k_out%d" % i)
+            k_out.append(k_tile)
 
-        quantise_b(0)
+        work = [(kind, store) for kind in (NOPE, VALUE) for store in range(STORES)]
+
+        def quantise_b_for(kind, store):
+            for chunk in range(store * CHUNKS_OF_STORE, (store + 1) * CHUNKS_OF_STORE):
+                quantise_b(chunk, kind)
+
+        quantise_b_for(NOPE, 0)
         norm_factor(0)
         norm_factor(1)
         quantise_cn(0)
         rotate_rope_key()
-        for i in range(TOKEN_TILES):
-            if i + 2 < TOKEN_TILES:
-                norm_factor(i + 2)
+        repeat_rope_key(0)
+        for i in range(1, TOKEN_TILES):
             if i + 1 < TOKEN_TILES:
-                quantise_cn(i + 1)
-            multiply_and_store(0, i)
-        for piece in range(1, PIECES):
-            quantise_b(piece)
+                norm_factor(i + 1)
+            quantise_cn(i)
+            repeat_rope_key(i)
+        for number, (kind, store) in enumerate(work):
             for i in range(TOKEN_TILES):
-                multiply_and_store(piece, i)
+                multiply_and_store(kind, store, i)
+            if number + 1 < len(work):
+                quantise_b_for(*work[number + 1])

@@ -114,7 +114,10 @@ def tile_mla_pb_kernel(tc, x, wkv_a, wkv_b, out_0, out_1):
         for g in range(A_PASSES):
             raw = keep.tile([P, PACK, A_COLS], BF16, name="a_raw%d" % g)
             rows = wkv_a[g * K_PASS : (g + 1) * K_PASS, :]
-            nc.sync.dma_start(out=raw[:], in_=rows.rearrange("(p t) c -> p t c", t=PACK))
+            nc.sync.dma_start(
+                out=raw[:].rearrange("p (u e) c -> p u (e c)", u=2),
+                in_=rows.rearrange("(u p e) c -> p u (e c)", u=2, e=2),
+            )
             a_raw.append(raw)
         b_raw = []
         for chunk in range(CHUNKS):
@@ -146,7 +149,7 @@ def tile_mla_pb_kernel(tc, x, wkv_a, wkv_b, out_0, out_1):
         b_scales = keep.tile([P, 2, HEADS, HEAD_DIM], U8, name="b_scales", align_bytes=64)
 
         for i in range(TOKEN_TILES):
-            words = x_raw[i][:].bitcast(F32).rearrange("p (g q u) -> p g u q", g=A_PASSES, u=2)
+            words = x_raw[i][:].bitcast(F32).rearrange("p (g u q) -> p g u q", g=A_PASSES, u=2)
             x_grouped = stage.tile([P, A_PASSES * P * PACK], BF16, name="x_grouped", align_bytes=64)
             grouped_words = x_grouped[:].bitcast(F32).rearrange(
                 "p (g w u) -> p g w u", g=A_PASSES, u=2

@@ -114,10 +114,7 @@ def tile_mla_pb_kernel(tc, x, wkv_a, wkv_b, out_0, out_1):
         for g in range(A_PASSES):
             raw = keep.tile([P, PACK, A_COLS], BF16, name="a_raw%d" % g)
             rows = wkv_a[g * K_PASS : (g + 1) * K_PASS, :]
-            nc.sync.dma_start(
-                out=raw[:].rearrange("p (u e) c -> p u (e c)", u=2),
-                in_=rows.rearrange("(u p e) c -> p u (e c)", u=2, e=2),
-            )
+            nc.sync.dma_start(out=raw[:], in_=rows.rearrange("(p t) c -> p t c", t=PACK))
             a_raw.append(raw)
         b_raw = []
         for chunk in range(CHUNKS):
@@ -148,9 +145,18 @@ def tile_mla_pb_kernel(tc, x, wkv_a, wkv_b, out_0, out_1):
         b_codes = keep.tile([P, 2, HEADS, HEAD_DIM], U32, name="b_codes", align_bytes=64)
         b_scales = keep.tile([P, 2, HEADS, HEAD_DIM], U8, name="b_scales", align_bytes=64)
 
+        def quantise_x(i, x_grouped):
+            nc.vector.quantize_mx(
+                out=x_codes[:, i, :, :].rearrange("p g w -> p (g w)").bitcast(FP8X4),
+                scales=x_scales[:, i, :, :].rearrange("p g w -> p (g w)"),
+                in_=x_grouped[:],
+            )
+
+        grouped_tiles = []
         for i in range(TOKEN_TILES):
-            words = x_raw[i][:].bitcast(F32).rearrange("p (g u q) -> p g u q", g=A_PASSES, u=2)
+            words = x_raw[i][:].bitcast(F32).rearrange("p (g q u) -> p g u q", g=A_PASSES, u=2)
             x_grouped = stage.tile([P, A_PASSES * P * PACK], BF16, name="x_grouped", align_bytes=64)
+            grouped_tiles.append(x_grouped)
             grouped_words = x_grouped[:].bitcast(F32).rearrange(
                 "p (g w u) -> p g w u", g=A_PASSES, u=2
             )
@@ -165,11 +171,9 @@ def tile_mla_pb_kernel(tc, x, wkv_a, wkv_b, out_0, out_1):
                     out=grouped_words[:, 2 * bank_no : 2 * bank_no + 2, :, :],
                     in_=x_bank[:].rearrange("p g u w -> p g w u"),
                 )
-            nc.vector.quantize_mx(
-                out=x_codes[:, i, :, :].rearrange("p g w -> p (g w)").bitcast(FP8X4),
-                scales=x_scales[:, i, :, :].rearrange("p g w -> p (g w)"),
-                in_=x_grouped[:],
-            )
+            if i > 0:
+                quantise_x(i - 1, grouped_tiles[i - 1])
+        quantise_x(TOKEN_TILES - 1, grouped_tiles[TOKEN_TILES - 1])
 
         c_banks = []
         for i in range(TOKEN_TILES):
@@ -217,33 +221,38 @@ def tile_mla_pb_kernel(tc, x, wkv_a, wkv_b, out_0, out_1):
                     stop=(g == A_PASSES - 1),
                 )
 
-        def quantise_b(chunk, kind):
-            b_grouped = b_stage.tile(
-                [P, CHUNK_HEADS * HEAD_DIM, PACK], BF16, name="b_grouped", align_bytes=64
-            )
-            nc.vector.tensor_copy(
-                out=b_grouped[:].rearrange("p (h c i) t -> p h c t i", h=CHUNK_HEADS, i=RUN),
-                in_=b_raw[chunk][:, :, :, kind, :].rearrange("p t h (c i) -> p h c t i", i=RUN),
-            )
-            heads = slice(chunk * CHUNK_HEADS, (chunk + 1) * CHUNK_HEADS)
-            nc.vector.quantize_mx(
-                out=b_codes[:, kind, heads, :].rearrange("p h d -> p (h d)").bitcast(FP8X4),
-                scales=b_scales[:, kind, heads, :].rearrange("p h d -> p (h d)"),
-                in_=b_grouped[:].rearrange("p c t -> p (c t)"),
-            )
+        def quantise_b(kind, store):
+            chunks = range(store * CHUNKS_OF_STORE, (store + 1) * CHUNKS_OF_STORE)
+            grouped_chunks = []
+            for chunk in chunks:
+                b_grouped = b_stage.tile(
+                    [P, CHUNK_HEADS * HEAD_DIM, PACK], BF16, name="b_grouped", align_bytes=64
+                )
+                nc.vector.tensor_copy(
+                    out=b_grouped[:].rearrange("p (h c i) t -> p h c t i", h=CHUNK_HEADS, i=RUN),
+                    in_=b_raw[chunk][:, :, :, kind, :].rearrange("p t h (c i) -> p h c t i", i=RUN),
+                )
+                grouped_chunks.append(b_grouped)
+            for chunk, b_grouped in zip(chunks, grouped_chunks):
+                heads = slice(chunk * CHUNK_HEADS, (chunk + 1) * CHUNK_HEADS)
+                nc.vector.quantize_mx(
+                    out=b_codes[:, kind, heads, :].rearrange("p h d -> p (h d)").bitcast(FP8X4),
+                    scales=b_scales[:, kind, heads, :].rearrange("p h d -> p (h d)"),
+                    in_=b_grouped[:].rearrange("p c t -> p (c t)"),
+                )
 
-        def rotate_rope_key():
-            halves = TOKEN_TILES * 2
-            products = keep.tile([P, 2, halves, HALF], F32, name="products")
+        def multiply_rope_key():
             nc.vector.tensor_tensor(
                 out=products[:],
                 in0=r_bank[:]
                 .rearrange("p i (h j) -> p (i h) j", j=HALF)
                 .unsqueeze(1)
-                .to_broadcast([P, 2, halves, HALF]),
-                in1=trig[:].unsqueeze(2).to_broadcast([P, 2, halves, HALF]),
+                .to_broadcast([P, 2, 2 * TOKEN_TILES, HALF]),
+                in1=trig[:].unsqueeze(2).to_broadcast([P, 2, 2 * TOKEN_TILES, HALF]),
                 op=ALU.mult,
             )
+
+        def rotate_rope_key():
             by_half = products[:].rearrange("p f (i h) j -> p f i h j", h=2)
             nc.vector.tensor_tensor(
                 out=rope[:, :, 0, :],
@@ -258,21 +267,24 @@ def tile_mla_pb_kernel(tc, x, wkv_a, wkv_b, out_0, out_1):
                 op=ALU.add,
             )
 
-        def norm_factor(i):
-            one = slice(i, i + 1)
-            squares = stage.tile([P, LATENT], F32, name="squares")
+        def norm_factors():
+            for i in range(TOKEN_TILES):
+                squares = stage.tile([P, LATENT], F32, name="squares")
+                nc.scalar.activation(
+                    out=squares[:],
+                    in_=c_banks[i][:],
+                    func=ACT.Square,
+                    accum_out=sum_squares[:, i : i + 1],
+                )
             nc.scalar.activation(
-                out=squares[:], in_=c_banks[i][:], func=ACT.Square, accum_out=sum_squares[:, one]
-            )
-            nc.scalar.activation(
-                out=inv_rms[:, one],
-                in_=sum_squares[:, one],
+                out=inv_rms[:],
+                in_=sum_squares[:],
                 func=ACT.Abs_reciprocal_sqrt,
                 scale=1.0 / LATENT,
                 bias=eps[:],
             )
 
-        def quantise_cn(i):
+        def transpose_cn(i):
             cn = stage.tile([P, PACK, P], BF16, name="cn")
             nc.scalar.activation(
                 out=cn[:],
@@ -285,6 +297,9 @@ def tile_mla_pb_kernel(tc, x, wkv_a, wkv_b, out_0, out_1):
                 nc.tensor.transpose(cn_bank[:, t, :], cn[:, t, :], ident_bf16[:])
             cn_grouped = stage.tile([P, P, PACK], BF16, name="cn_grouped", align_bytes=64)
             nc.vector.tensor_copy(out=cn_grouped[:], in_=cn_bank[:].rearrange("p t w -> p w t"))
+            return cn_grouped
+
+        def quantise_cn(i, cn_grouped):
             nc.vector.quantize_mx(
                 out=cn_codes[:, i, :].bitcast(FP8X4),
                 scales=cn_scales[:, i, :],
@@ -327,6 +342,7 @@ def tile_mla_pb_kernel(tc, x, wkv_a, wkv_b, out_0, out_1):
                 in_=out_tile[:, :, 0:width],
             )
 
+        products = keep.tile([P, 2, 2 * TOKEN_TILES, HALF], F32, name="products")
         rope = keep.tile([P, TOKEN_TILES, 2, HALF], F32, name="rope")
         sum_squares = keep.tile([P, TOKEN_TILES], F32, name="sum_squares")
         inv_rms = keep.tile([P, TOKEN_TILES], F32, name="inv_rms")
@@ -337,23 +353,19 @@ def tile_mla_pb_kernel(tc, x, wkv_a, wkv_b, out_0, out_1):
 
         work = [(kind, store) for kind in (NOPE, VALUE) for store in range(STORES)]
 
-        def quantise_b_for(kind, store):
-            for chunk in range(store * CHUNKS_OF_STORE, (store + 1) * CHUNKS_OF_STORE):
-                quantise_b(chunk, kind)
-
-        quantise_b_for(NOPE, 0)
-        norm_factor(0)
-        norm_factor(1)
-        quantise_cn(0)
+        norm_factors()
+        quantise_b(*work[0])
+        multiply_rope_key()
+        cn_grouped = transpose_cn(0)
         rotate_rope_key()
-        repeat_rope_key(0)
+        quantise_cn(0, cn_grouped)
         for i in range(1, TOKEN_TILES):
-            if i + 1 < TOKEN_TILES:
-                norm_factor(i + 1)
-            quantise_cn(i)
-            repeat_rope_key(i)
+            cn_grouped = transpose_cn(i)
+            repeat_rope_key(i - 1)
+            quantise_cn(i, cn_grouped)
+        repeat_rope_key(TOKEN_TILES - 1)
         for number, (kind, store) in enumerate(work):
             for i in range(TOKEN_TILES):
                 multiply_and_store(kind, store, i)
             if number + 1 < len(work):
-                quantise_b_for(*work[number + 1])
+                quantise_b(*work[number + 1])

@@ -16,7 +16,6 @@ ACT = mybir.ActivationFunctionType
 P = 128
 PACK = 4
 K_PASS = P * PACK
-PSUM_BANKS = 8
 
 TOKENS = 512
 TOKEN_TILES = TOKENS // P
@@ -25,8 +24,6 @@ A_PASSES = DIM // K_PASS
 LATENT = 512
 ROPE_DIM = 128
 HALF = ROPE_DIM // 2
-DOUBLINGS = 6
-assert 2**DOUBLINGS == HALF
 A_COLS = LATENT + ROPE_DIM
 HEADS = 16
 HEAD_DIM = 128
@@ -39,12 +36,15 @@ CHUNKS = HEADS // CHUNK_HEADS
 CHUNK_COLS = CHUNK_HEADS * 2 * HEAD_DIM
 NOPE = 0
 VALUE = 1
-STORE_HEADS = 2 * CHUNK_HEADS
-STORES = HEADS // STORE_HEADS
-CHUNKS_OF_STORE = STORE_HEADS // CHUNK_HEADS
-A_VECTOR_COLS = A_COLS // 2
+A_VECTOR_COLS = 384
+TRIG_VECTOR = 72
 RUN = 4
-V_BUFS = 4
+C_BANKS = (0, 1, 2, 3)
+X_BANKS = (4, 5)
+R_BANK = 6
+CN_BANKS = (7, 4)
+V_BUFS = 8
+K_SLOTS = 2
 
 FLOPS = 2 * TOKENS * DIM * A_COLS + 2 * TOKENS * LATENT * HEADS * 2 * HEAD_DIM
 
@@ -57,37 +57,24 @@ def regroup(copy, grouped, raw):
 
 
 def build_rope_table(nc, pool):
-    theta = pool.tile([P, HALF], F32, name="theta")
-    nc.vector.memset(theta[:, 0:1], 1.0)
-    for step in range(DOUBLINGS):
-        width = 2**step
-        nc.vector.tensor_scalar(
-            out=theta[:, width : 2 * width],
-            in0=theta[:, 0:width],
-            scalar1=ROPE_BASE ** (-width / HALF),
-            scalar2=None,
-            op0=ALU.mult,
-        )
-    turns = pool.tile([P, 2, HALF], F32, name="turns")
-    per_turn = POSITION / (2.0 * math.pi)
-    nc.vector.tensor_scalar(
-        out=turns[:, 0, :], in0=theta[:], scalar1=per_turn, scalar2=0.25, op0=ALU.mult, op1=ALU.add
-    )
-    nc.vector.tensor_scalar(
-        out=turns[:, 1, :], in0=theta[:], scalar1=per_turn, scalar2=None, op0=ALU.mult
-    )
-    whole_int = pool.tile([P, 2, HALF], I32, name="whole_int")
-    nc.vector.tensor_copy(out=whole_int[:], in_=turns[:])
-    whole = pool.tile([P, 2, HALF], F32, name="whole")
-    nc.vector.tensor_copy(out=whole[:], in_=whole_int[:])
-    left = pool.tile([P, 2, HALF], F32, name="left")
-    nc.vector.tensor_tensor(out=left[:], in0=turns[:], in1=whole[:], op=ALU.subtract)
-    minus = pool.tile([P, 2, HALF], F32, name="minus")
-    nc.vector.scalar_tensor_tensor(
-        out=minus[:], in0=left[:], scalar=0.5, in1=left[:], op0=ALU.is_gt, op1=ALU.subtract
-    )
     trig = pool.tile([P, 2, HALF], F32, name="trig")
-    nc.scalar.activation(out=trig[:], in_=minus[:], func=ACT.Sin, scale=-2.0 * math.pi)
+
+    def fill(engine, name, first, last):
+        one = pool.tile([P, 1], F32, name=name)
+        engine.memset(one[:], 1.0)
+        for n in range(first, last):
+            f, j = divmod(n, HALF)
+            angle = POSITION * ROPE_BASE ** (-j / HALF)
+            engine.tensor_scalar(
+                out=trig[:, f, j : j + 1],
+                in0=one[:],
+                scalar1=(math.cos, math.sin)[f](angle),
+                scalar2=None,
+                op0=ALU.mult,
+            )
+
+    fill(nc.vector, "one_v", 0, TRIG_VECTOR)
+    fill(nc.gpsimd, "one_g", TRIG_VECTOR, 2 * HALF)
     return trig
 
 
@@ -101,30 +88,39 @@ def tile_mla_pb_kernel(tc, x, wkv_a, wkv_b, out_0, out_1):
         stack.enter_context(tc.manual_schedule())
         keep = stack.enter_context(tc.tile_pool(name="keep", bufs=1))
         stage = stack.enter_context(tc.tile_pool(name="stage", bufs=2))
-        b_stage = stack.enter_context(tc.tile_pool(name="b_stage", bufs=4))
+        b_stage = stack.enter_context(tc.tile_pool(name="b_stage", bufs=2))
         outs = stack.enter_context(tc.tile_pool(name="outs", bufs=V_BUFS))
-        psum = stack.enter_context(tc.psum_pool(name="psum", bufs=PSUM_BANKS))
+        psum = stack.enter_context(tc.psum_pool(name="psum", bufs=1))
 
-        x_raw = []
-        for i in range(TOKEN_TILES):
+        x_raw = [None] * TOKEN_TILES
+        a_raw = [None] * A_PASSES
+        b_raw = [None] * CHUNKS
+
+        def load_x(i):
             raw = keep.tile([P, DIM], BF16, name="x_raw%d" % i)
             nc.sync.dma_start(out=raw[:], in_=x_rows[i * P : (i + 1) * P, :])
-            x_raw.append(raw)
-        a_raw = []
-        for g in range(A_PASSES):
+            x_raw[i] = raw
+
+        def load_a(g):
             raw = keep.tile([P, PACK, A_COLS], BF16, name="a_raw%d" % g)
             rows = wkv_a[g * K_PASS : (g + 1) * K_PASS, :]
             nc.sync.dma_start(out=raw[:], in_=rows.rearrange("(p t) c -> p t c", t=PACK))
-            a_raw.append(raw)
-        b_raw = []
-        for chunk in range(CHUNKS):
+            a_raw[g] = raw
+
+        def load_b(chunk):
             raw = keep.tile([P, PACK, CHUNK_HEADS, 2, HEAD_DIM], BF16, name="b_raw%d" % chunk)
             cols = wkv_b[:, chunk * CHUNK_COLS : (chunk + 1) * CHUNK_COLS]
             nc.sync.dma_start(
                 out=raw[:].rearrange("p t h f d -> p t (h f d)"),
                 in_=cols.rearrange("(p t) c -> p t c", t=PACK),
             )
-            b_raw.append(raw)
+            b_raw[chunk] = raw
+
+        for n in range(TOKEN_TILES):
+            load_a(n)
+            load_x(n)
+        for chunk in range(CHUNKS):
+            load_b(chunk)
 
         ident_f32 = keep.tile([P, P], F32, name="ident_f32")
         make_identity(nc, ident_f32[:])
@@ -145,6 +141,42 @@ def tile_mla_pb_kernel(tc, x, wkv_a, wkv_b, out_0, out_1):
         b_codes = keep.tile([P, 2, HEADS, HEAD_DIM], U32, name="b_codes", align_bytes=64)
         b_scales = keep.tile([P, 2, HEADS, HEAD_DIM], U8, name="b_scales", align_bytes=64)
 
+        def bank_tile(shape, dtype, number):
+            bank = psum.tile(shape, dtype, name="bank%d" % number)
+            return bank
+
+        sum_squares = keep.tile([P, TOKEN_TILES], F32, name="sum_squares")
+        inv_rms = keep.tile([P, TOKEN_TILES], F32, name="inv_rms")
+        products = keep.tile([P, 2, 2 * TOKEN_TILES, HALF], F32, name="products")
+        rope = keep.tile([P, TOKEN_TILES, 2, HALF], F32, name="rope")
+        c_banks = {}
+        r_bank = bank_tile([P, TOKEN_TILES, ROPE_DIM], F32, R_BANK)
+        k_out = []
+        for i in range(TOKEN_TILES):
+            k_tile = keep.tile(
+                [P, K_SLOTS, CHUNK_HEADS, HEAD_DIM + ROPE_DIM], F32, name="k_out%d" % i
+            )
+            k_out.append(k_tile)
+
+        def transpose_x(i, copies):
+            words = x_raw[i][:].bitcast(F32).rearrange("p (g q u) -> p g u q", g=A_PASSES, u=2)
+            x_grouped = stage.tile([P, A_PASSES * P * PACK], BF16, name="x_grouped", align_bytes=64)
+            grouped_words = x_grouped[:].bitcast(F32).rearrange(
+                "p (g w u) -> p g w u", g=A_PASSES, u=2
+            )
+            for half, copy in enumerate(copies):
+                x_bank = bank_tile([P, 2, 2, P], F32, X_BANKS[half])
+                for g in range(2):
+                    for u in range(2):
+                        nc.tensor.transpose(
+                            x_bank[:, g, u, :], words[:, 2 * half + g, u, :], ident_f32[:]
+                        )
+                copy(
+                    out=grouped_words[:, 2 * half : 2 * half + 2, :, :],
+                    in_=x_bank[:].rearrange("p g u w -> p g w u"),
+                )
+            return x_grouped
+
         def quantise_x(i, x_grouped):
             nc.vector.quantize_mx(
                 out=x_codes[:, i, :, :].rearrange("p g w -> p (g w)").bitcast(FP8X4),
@@ -152,34 +184,7 @@ def tile_mla_pb_kernel(tc, x, wkv_a, wkv_b, out_0, out_1):
                 in_=x_grouped[:],
             )
 
-        grouped_tiles = []
-        for i in range(TOKEN_TILES):
-            words = x_raw[i][:].bitcast(F32).rearrange("p (g q u) -> p g u q", g=A_PASSES, u=2)
-            x_grouped = stage.tile([P, A_PASSES * P * PACK], BF16, name="x_grouped", align_bytes=64)
-            grouped_tiles.append(x_grouped)
-            grouped_words = x_grouped[:].bitcast(F32).rearrange(
-                "p (g w u) -> p g w u", g=A_PASSES, u=2
-            )
-            for bank_no, copy in enumerate((nc.scalar.copy, nc.vector.tensor_copy)):
-                x_bank = psum.tile([P, 2, 2, P], F32, name="x_bank", tag="bank")
-                for g in range(2):
-                    for u in range(2):
-                        nc.tensor.transpose(
-                            x_bank[:, g, u, :], words[:, 2 * bank_no + g, u, :], ident_f32[:]
-                        )
-                copy(
-                    out=grouped_words[:, 2 * bank_no : 2 * bank_no + 2, :, :],
-                    in_=x_bank[:].rearrange("p g u w -> p g w u"),
-                )
-            if i > 0:
-                quantise_x(i - 1, grouped_tiles[i - 1])
-        quantise_x(TOKEN_TILES - 1, grouped_tiles[TOKEN_TILES - 1])
-
-        c_banks = []
-        for i in range(TOKEN_TILES):
-            c_bank = psum.tile([P, LATENT], F32, name="c_bank%d" % i, tag="bank")
-            c_banks.append(c_bank)
-        for g in range(A_PASSES):
+        def regroup_a(g):
             a_grouped = stage.tile([P, A_COLS, PACK], BF16, name="a_grouped", align_bytes=64)
             regroup(
                 nc.vector.tensor_copy,
@@ -191,55 +196,84 @@ def tile_mla_pb_kernel(tc, x, wkv_a, wkv_b, out_0, out_1):
                 a_grouped[:, A_VECTOR_COLS:A_COLS, :],
                 a_raw[g][:, :, A_VECTOR_COLS:A_COLS],
             )
+            return a_grouped
+
+        def quantise_a(g, a_grouped):
             for first, last in ((0, LATENT), (LATENT, A_COLS)):
                 nc.vector.quantize_mx(
                     out=a_codes[:, g, first:last].bitcast(FP8X4),
                     scales=a_scales[:, g, first:last],
                     in_=a_grouped[:, first:last, :].rearrange("p c t -> p (c t)"),
                 )
-            for i in range(TOKEN_TILES):
-                nc.tensor.matmul_mx(
-                    out=c_banks[i][:],
-                    lhsT=x_codes[:, i, g, :].bitcast(FP8X4),
-                    lhsT_scale=x_scales[:, i, g, :],
-                    rhs=a_codes[:, g, 0:LATENT].bitcast(FP8X4),
-                    rhs_scale=a_scales[:, g, 0:LATENT],
-                    start=(g == 0),
-                    stop=(g == A_PASSES - 1),
-                )
 
-        r_bank = psum.tile([P, TOKEN_TILES, ROPE_DIM], F32, name="r_bank", tag="bank")
-        for i in range(TOKEN_TILES):
-            for g in range(A_PASSES):
-                nc.tensor.matmul_mx(
-                    out=r_bank[:, i, :],
-                    lhsT=x_codes[:, i, g, :].bitcast(FP8X4),
-                    lhsT_scale=x_scales[:, i, g, :],
-                    rhs=a_codes[:, g, LATENT:A_COLS].bitcast(FP8X4),
-                    rhs_scale=a_scales[:, g, LATENT:A_COLS],
-                    start=(g == 0),
-                    stop=(g == A_PASSES - 1),
-                )
+        def c_pass(i, g):
+            if g == 0:
+                c_banks[i] = bank_tile([P, LATENT], F32, C_BANKS[i])
+            nc.tensor.matmul_mx(
+                out=c_banks[i][:],
+                lhsT=x_codes[:, i, g, :].bitcast(FP8X4),
+                lhsT_scale=x_scales[:, i, g, :],
+                rhs=a_codes[:, g, 0:LATENT].bitcast(FP8X4),
+                rhs_scale=a_scales[:, g, 0:LATENT],
+                start=(g == 0),
+                stop=(g == A_PASSES - 1),
+            )
 
-        def quantise_b(kind, store):
-            chunks = range(store * CHUNKS_OF_STORE, (store + 1) * CHUNKS_OF_STORE)
-            grouped_chunks = []
-            for chunk in chunks:
-                b_grouped = b_stage.tile(
-                    [P, CHUNK_HEADS * HEAD_DIM, PACK], BF16, name="b_grouped", align_bytes=64
-                )
-                nc.vector.tensor_copy(
-                    out=b_grouped[:].rearrange("p (h c i) t -> p h c t i", h=CHUNK_HEADS, i=RUN),
-                    in_=b_raw[chunk][:, :, :, kind, :].rearrange("p t h (c i) -> p h c t i", i=RUN),
-                )
-                grouped_chunks.append(b_grouped)
-            for chunk, b_grouped in zip(chunks, grouped_chunks):
-                heads = slice(chunk * CHUNK_HEADS, (chunk + 1) * CHUNK_HEADS)
-                nc.vector.quantize_mx(
-                    out=b_codes[:, kind, heads, :].rearrange("p h d -> p (h d)").bitcast(FP8X4),
-                    scales=b_scales[:, kind, heads, :].rearrange("p h d -> p (h d)"),
-                    in_=b_grouped[:].rearrange("p c t -> p (c t)"),
-                )
+        def multiply_r(tiles):
+            for i in tiles:
+                for g in range(A_PASSES):
+                    nc.tensor.matmul_mx(
+                        out=r_bank[:, i, :],
+                        lhsT=x_codes[:, i, g, :].bitcast(FP8X4),
+                        lhsT_scale=x_scales[:, i, g, :],
+                        rhs=a_codes[:, g, LATENT:A_COLS].bitcast(FP8X4),
+                        rhs_scale=a_scales[:, g, LATENT:A_COLS],
+                        start=(g == 0),
+                        stop=(g == A_PASSES - 1),
+                    )
+
+        def square_c(i):
+            squares = stage.tile([P, LATENT], F32, name="squares")
+            nc.scalar.activation(
+                out=squares[:],
+                in_=c_banks[i][:],
+                func=ACT.Square,
+                accum_out=sum_squares[:, i : i + 1],
+            )
+
+        def norm_factors(tiles):
+            nc.scalar.activation(
+                out=inv_rms[:, tiles],
+                in_=sum_squares[:, tiles],
+                func=ACT.Abs_reciprocal_sqrt,
+                scale=1.0 / LATENT,
+                bias=eps[:],
+            )
+
+        def scale_c(i):
+            cn = stage.tile([P, PACK, P], BF16, name="cn")
+            nc.scalar.activation(
+                out=cn[:],
+                in_=c_banks[i][:].rearrange("p (q t) -> p t q", t=PACK),
+                func=ACT.Copy,
+                scale=inv_rms[:, i : i + 1],
+            )
+            return cn
+
+        def transpose_cn(i, cn, copy):
+            cn_bank = bank_tile([P, PACK, P], BF16, CN_BANKS[i % 2])
+            for t in range(PACK):
+                nc.tensor.transpose(cn_bank[:, t, :], cn[:, t, :], ident_bf16[:])
+            cn_grouped = stage.tile([P, P, PACK], BF16, name="cn_grouped", align_bytes=64)
+            copy(out=cn_grouped[:], in_=cn_bank[:].rearrange("p t w -> p w t"))
+            return cn_grouped
+
+        def quantise_cn(i, cn_grouped):
+            nc.vector.quantize_mx(
+                out=cn_codes[:, i, :].bitcast(FP8X4),
+                scales=cn_scales[:, i, :],
+                in_=cn_grouped[:].rearrange("p w t -> p (w t)"),
+            )
 
         def multiply_rope_key():
             nc.vector.tensor_tensor(
@@ -267,105 +301,125 @@ def tile_mla_pb_kernel(tc, x, wkv_a, wkv_b, out_0, out_1):
                 op=ALU.add,
             )
 
-        def norm_factors():
-            for i in range(TOKEN_TILES):
-                squares = stage.tile([P, LATENT], F32, name="squares")
-                nc.scalar.activation(
-                    out=squares[:],
-                    in_=c_banks[i][:],
-                    func=ACT.Square,
-                    accum_out=sum_squares[:, i : i + 1],
-                )
-            nc.scalar.activation(
-                out=inv_rms[:],
-                in_=sum_squares[:],
-                func=ACT.Abs_reciprocal_sqrt,
-                scale=1.0 / LATENT,
-                bias=eps[:],
-            )
-
-        def transpose_cn(i):
-            cn = stage.tile([P, PACK, P], BF16, name="cn")
-            nc.scalar.activation(
-                out=cn[:],
-                in_=c_banks[i][:].rearrange("p (q t) -> p t q", t=PACK),
-                func=ACT.Copy,
-                scale=inv_rms[:, i : i + 1],
-            )
-            cn_bank = psum.tile([P, PACK, P], BF16, name="cn_bank", tag="bank")
-            for t in range(PACK):
-                nc.tensor.transpose(cn_bank[:, t, :], cn[:, t, :], ident_bf16[:])
-            cn_grouped = stage.tile([P, P, PACK], BF16, name="cn_grouped", align_bytes=64)
-            nc.vector.tensor_copy(out=cn_grouped[:], in_=cn_bank[:].rearrange("p t w -> p w t"))
-            return cn_grouped
-
-        def quantise_cn(i, cn_grouped):
-            nc.vector.quantize_mx(
-                out=cn_codes[:, i, :].bitcast(FP8X4),
-                scales=cn_scales[:, i, :],
-                in_=cn_grouped[:].rearrange("p w t -> p (w t)"),
-            )
-
-        def repeat_rope_key(i):
+        def repeat_rope_key(i, slot):
             nc.vector.tensor_copy(
-                out=k_out[i][:, :, HEAD_DIM : HEAD_DIM + ROPE_DIM],
+                out=k_out[i][:, slot, :, HEAD_DIM : HEAD_DIM + ROPE_DIM],
                 in_=rope[:, i, :, :]
                 .rearrange("p h j -> p (h j)")
                 .unsqueeze(1)
-                .to_broadcast([P, STORE_HEADS, ROPE_DIM]),
+                .to_broadcast([P, CHUNK_HEADS, ROPE_DIM]),
             )
 
-        def multiply_and_store(kind, store, i):
-            if kind == NOPE:
-                out_tile, out_rows, width = k_out[i], k_rows, HEAD_DIM + ROPE_DIM
-            else:
-                out_tile = outs.tile([P, STORE_HEADS, HEAD_DIM], F32, name="v_out")
-                out_rows, width = v_rows, HEAD_DIM
-            first_head = store * STORE_HEADS
-            for first in range(0, STORE_HEADS, CHUNK_HEADS):
-                u_bank = psum.tile([P, CHUNK_HEADS, HEAD_DIM], F32, name="u_bank", tag="bank")
-                for h in range(CHUNK_HEADS):
-                    nc.tensor.matmul_mx(
-                        out=u_bank[:, h, :],
-                        lhsT=cn_codes[:, i, :].bitcast(FP8X4),
-                        lhsT_scale=cn_scales[:, i, :],
-                        rhs=b_codes[:, kind, first_head + first + h, :].bitcast(FP8X4),
-                        rhs_scale=b_scales[:, kind, first_head + first + h, :],
-                        start=True,
-                        stop=True,
-                    )
-                nc.scalar.copy(
-                    out=out_tile[:, first : first + CHUNK_HEADS, 0:HEAD_DIM], in_=u_bank[:]
+        def regroup_b(kind, chunk):
+            b_grouped = b_stage.tile(
+                [P, CHUNK_HEADS * HEAD_DIM, PACK], BF16, name="b_grouped", align_bytes=64
+            )
+            nc.vector.tensor_copy(
+                out=b_grouped[:].rearrange("p (h c i) t -> p h c t i", h=CHUNK_HEADS, i=RUN),
+                in_=b_raw[chunk][:, :, :, kind, :].rearrange("p t h (c i) -> p h c t i", i=RUN),
+            )
+            return b_grouped
+
+        def quantise_b(kind, chunk, b_grouped):
+            heads = slice(chunk * CHUNK_HEADS, (chunk + 1) * CHUNK_HEADS)
+            nc.vector.quantize_mx(
+                out=b_codes[:, kind, heads, :].rearrange("p h d -> p (h d)").bitcast(FP8X4),
+                scales=b_scales[:, kind, heads, :].rearrange("p h d -> p (h d)"),
+                in_=b_grouped[:].rearrange("p c t -> p (c t)"),
+            )
+
+        def multiply_b(kind, chunk, i, number):
+            u_bank = bank_tile([P, CHUNK_HEADS, HEAD_DIM], F32, number)
+            for h in range(CHUNK_HEADS):
+                nc.tensor.matmul_mx(
+                    out=u_bank[:, h, :],
+                    lhsT=cn_codes[:, i, :].bitcast(FP8X4),
+                    lhsT_scale=cn_scales[:, i, :],
+                    rhs=b_codes[:, kind, chunk * CHUNK_HEADS + h, :].bitcast(FP8X4),
+                    rhs_scale=b_scales[:, kind, chunk * CHUNK_HEADS + h, :],
+                    start=True,
+                    stop=True,
                 )
+            return u_bank
+
+        def store(kind, chunk, i, u_bank, copy):
+            if kind == NOPE:
+                out_heads = k_out[i][:, chunk % K_SLOTS, :, :]
+                out_rows, width = k_rows, HEAD_DIM + ROPE_DIM
+            else:
+                v_out = outs.tile([P, CHUNK_HEADS, HEAD_DIM], F32, name="v_out")
+                out_heads, out_rows, width = v_out[:], v_rows, HEAD_DIM
+            copy(out=out_heads[:, :, 0:HEAD_DIM], in_=u_bank[:])
+            heads = slice(chunk * CHUNK_HEADS, (chunk + 1) * CHUNK_HEADS)
             nc.sync.dma_start(
-                out=out_rows[i * P : (i + 1) * P, first_head : first_head + STORE_HEADS, :],
-                in_=out_tile[:, :, 0:width],
+                out=out_rows[i * P : (i + 1) * P, heads, :], in_=out_heads[:, :, 0:width]
             )
 
-        products = keep.tile([P, 2, 2 * TOKEN_TILES, HALF], F32, name="products")
-        rope = keep.tile([P, TOKEN_TILES, 2, HALF], F32, name="rope")
-        sum_squares = keep.tile([P, TOKEN_TILES], F32, name="sum_squares")
-        inv_rms = keep.tile([P, TOKEN_TILES], F32, name="inv_rms")
-        k_out = []
-        for i in range(TOKEN_TILES):
-            k_tile = keep.tile([P, STORE_HEADS, HEAD_DIM + ROPE_DIM], F32, name="k_out%d" % i)
-            k_out.append(k_tile)
-
-        work = [(kind, store) for kind in (NOPE, VALUE) for store in range(STORES)]
-
-        norm_factors()
-        quantise_b(*work[0])
+        V, A = nc.vector.tensor_copy, nc.scalar.copy
+        a_grouped = regroup_a(0)
+        x_grouped = transpose_x(0, (A, A))
+        for n in range(TOKEN_TILES):
+            last = n + 1 == TOKEN_TILES
+            quantise_a(n, a_grouped)
+            for i in range(n):
+                c_pass(i, n)
+            if not last:
+                a_grouped = regroup_a(n + 1)
+            quantise_x(n, x_grouped)
+            if last:
+                multiply_r(range(n))
+            else:
+                x_grouped = transpose_x(n + 1, (A, A))
+            for g in range(n + 1):
+                c_pass(n, g)
+        multiply_r([TOKEN_TILES - 1])
+        bg = regroup_b(NOPE, 0)
+        square_c(0)
+        square_c(1)
+        norm_factors(slice(0, 2))
+        cn0 = scale_c(0)
+        quantise_b(NOPE, 0, bg)
+        cn1 = scale_c(1)
         multiply_rope_key()
-        cn_grouped = transpose_cn(0)
+        cg0 = transpose_cn(0, cn0, V)
+        cg1 = transpose_cn(1, cn1, V)
+        quantise_cn(0, cg0)
+        quantise_cn(1, cg1)
         rotate_rope_key()
-        quantise_cn(0, cn_grouped)
-        for i in range(1, TOKEN_TILES):
-            cn_grouped = transpose_cn(i)
-            repeat_rope_key(i - 1)
-            quantise_cn(i, cn_grouped)
-        repeat_rope_key(TOKEN_TILES - 1)
-        for number, (kind, store) in enumerate(work):
+        square_c(2)
+        square_c(3)
+        norm_factors(slice(2, 4))
+        u0 = multiply_b(NOPE, 0, 0, 5)
+        u1 = multiply_b(NOPE, 0, 1, 6)
+        cn2 = scale_c(2)
+        cn3 = scale_c(3)
+        repeat_rope_key(0, 0)
+        store(NOPE, 0, 0, u0, A)
+        cg2 = transpose_cn(2, cn2, V)
+        repeat_rope_key(1, 0)
+        store(NOPE, 0, 1, u1, A)
+        cg3 = transpose_cn(3, cn3, V)
+        quantise_cn(2, cg2)
+        quantise_cn(3, cg3)
+        bg = regroup_b(NOPE, 1)
+        repeat_rope_key(2, 0)
+        u = multiply_b(NOPE, 0, 2, 0)
+        store(NOPE, 0, 2, u, A)
+        repeat_rope_key(3, 0)
+        u = multiply_b(NOPE, 0, 3, 1)
+        store(NOPE, 0, 3, u, A)
+        quantise_b(NOPE, 1, bg)
+        for i in range(TOKEN_TILES):
+            repeat_rope_key(i, 1)
+        number = 2
+        items = [(NOPE, 1), (NOPE, 2), (NOPE, 3), (VALUE, 0), (VALUE, 1), (VALUE, 2), (VALUE, 3)]
+        bg = regroup_b(*items[1])
+        for k, (kind, chunk) in enumerate(items):
             for i in range(TOKEN_TILES):
-                multiply_and_store(kind, store, i)
-            if number + 1 < len(work):
-                quantise_b(*work[number + 1])
+                u = multiply_b(kind, chunk, i, number % 8)
+                store(kind, chunk, i, u, A)
+                number += 1
+                if i == 0 and k + 1 < len(items):
+                    quantise_b(*items[k + 1], bg)
+                if i == 0 and k + 2 < len(items):
+                    bg = regroup_b(*items[k + 2])

@@ -24,6 +24,8 @@ A_PASSES = DIM // K_PASS
 LATENT = 512
 ROPE_DIM = 128
 HALF = ROPE_DIM // 2
+DOUBLINGS = 6
+assert 2**DOUBLINGS == HALF
 A_COLS = LATENT + ROPE_DIM
 HEADS = 16
 HEAD_DIM = 128
@@ -37,14 +39,14 @@ CHUNK_COLS = CHUNK_HEADS * 2 * HEAD_DIM
 NOPE = 0
 VALUE = 1
 A_VECTOR_COLS = 384
-TRIG_VECTOR = 72
+ROPE_STEPS_FIRST = 8
 RUN = 4
 C_BANKS = (0, 1, 2, 3)
 X_BANKS = (4, 5)
 R_BANK = 6
 CN_BANKS = (7, 4)
-V_BUFS = 8
-K_SLOTS = 2
+U_BUFS = 24
+PAIR = 2
 
 FLOPS = 2 * TOKENS * DIM * A_COLS + 2 * TOKENS * LATENT * HEADS * 2 * HEAD_DIM
 
@@ -56,26 +58,54 @@ def regroup(copy, grouped, raw):
     )
 
 
-def build_rope_table(nc, pool):
+def rope_table_steps(nc, pool):
+    theta = pool.tile([P, HALF], F32, name="theta")
+    turns = pool.tile([P, 2, HALF], F32, name="turns")
+    whole_int = pool.tile([P, 2, HALF], I32, name="whole_int")
+    whole = pool.tile([P, 2, HALF], F32, name="whole")
+    left = pool.tile([P, 2, HALF], F32, name="left")
+    minus = pool.tile([P, 2, HALF], F32, name="minus")
     trig = pool.tile([P, 2, HALF], F32, name="trig")
+    per_turn = POSITION / (2.0 * math.pi)
 
-    def fill(engine, name, first, last):
-        one = pool.tile([P, 1], F32, name=name)
-        engine.memset(one[:], 1.0)
-        for n in range(first, last):
-            f, j = divmod(n, HALF)
-            angle = POSITION * ROPE_BASE ** (-j / HALF)
-            engine.tensor_scalar(
-                out=trig[:, f, j : j + 1],
-                in0=one[:],
-                scalar1=(math.cos, math.sin)[f](angle),
-                scalar2=None,
-                op0=ALU.mult,
-            )
+    def double(width):
+        nc.vector.tensor_scalar(
+            out=theta[:, width : 2 * width],
+            in0=theta[:, 0:width],
+            scalar1=ROPE_BASE ** (-width / HALF),
+            scalar2=None,
+            op0=ALU.mult,
+        )
 
-    fill(nc.vector, "one_v", 0, TRIG_VECTOR)
-    fill(nc.gpsimd, "one_g", TRIG_VECTOR, 2 * HALF)
-    return trig
+    def to_turns():
+        nc.vector.tensor_scalar(
+            out=turns[:, 0, :], in0=theta[:], scalar1=per_turn, scalar2=0.25, op0=ALU.mult, op1=ALU.add
+        )
+        nc.vector.tensor_scalar(
+            out=turns[:, 1, :], in0=theta[:], scalar1=per_turn, scalar2=None, op0=ALU.mult
+        )
+
+    def take_off_whole_turns():
+        nc.vector.tensor_tensor(out=left[:], in0=turns[:], in1=whole[:], op=ALU.subtract)
+
+    def fold():
+        nc.vector.scalar_tensor_tensor(
+            out=minus[:], in0=left[:], scalar=0.5, in1=left[:], op0=ALU.is_gt, op1=ALU.subtract
+        )
+
+    steps = [lambda: nc.vector.memset(theta[:, 0:1], 1.0)]
+    steps += [lambda width=2**n: double(width) for n in range(DOUBLINGS)]
+    steps += [
+        to_turns,
+        lambda: nc.vector.tensor_copy(out=whole_int[:], in_=turns[:]),
+        lambda: nc.vector.tensor_copy(out=whole[:], in_=whole_int[:]),
+        take_off_whole_turns,
+        fold,
+        lambda: nc.scalar.activation(
+            out=trig[:], in_=minus[:], func=ACT.Sin, scale=-2.0 * math.pi
+        ),
+    ]
+    return trig, steps
 
 
 def tile_mla_pb_kernel(tc, x, wkv_a, wkv_b, out_0, out_1):
@@ -89,7 +119,7 @@ def tile_mla_pb_kernel(tc, x, wkv_a, wkv_b, out_0, out_1):
         keep = stack.enter_context(tc.tile_pool(name="keep", bufs=1))
         stage = stack.enter_context(tc.tile_pool(name="stage", bufs=2))
         b_stage = stack.enter_context(tc.tile_pool(name="b_stage", bufs=2))
-        outs = stack.enter_context(tc.tile_pool(name="outs", bufs=V_BUFS))
+        outs = stack.enter_context(tc.tile_pool(name="outs", bufs=U_BUFS))
         psum = stack.enter_context(tc.psum_pool(name="psum", bufs=1))
 
         x_raw = [None] * TOKEN_TILES
@@ -128,9 +158,11 @@ def tile_mla_pb_kernel(tc, x, wkv_a, wkv_b, out_0, out_1):
         make_identity(nc, ident_bf16[:])
         eps = keep.tile([P, 1], F32, name="eps")
         nc.vector.memset(eps[:], EPS)
-        trig = build_rope_table(nc, keep)
-        warm_up = keep.tile([P, 1], F32, name="warm_up")
-        nc.scalar.activation(out=warm_up[:], in_=eps[:], func=ACT.Abs_reciprocal_sqrt)
+        trig, rope_steps = rope_table_steps(nc, keep)
+        for step in rope_steps[:ROPE_STEPS_FIRST]:
+            step()
+        warm_up = keep.tile([P, 2], F32, name="warm_up")
+        nc.scalar.activation(out=warm_up[:, 0:1], in_=eps[:], func=ACT.Sin)
 
         x_codes = keep.tile([P, TOKEN_TILES, A_PASSES, P], U32, name="x_codes", align_bytes=64)
         x_scales = keep.tile([P, TOKEN_TILES, A_PASSES, P], U8, name="x_scales", align_bytes=64)
@@ -147,16 +179,9 @@ def tile_mla_pb_kernel(tc, x, wkv_a, wkv_b, out_0, out_1):
 
         sum_squares = keep.tile([P, TOKEN_TILES], F32, name="sum_squares")
         inv_rms = keep.tile([P, TOKEN_TILES], F32, name="inv_rms")
-        products = keep.tile([P, 2, 2 * TOKEN_TILES, HALF], F32, name="products")
         rope = keep.tile([P, TOKEN_TILES, 2, HALF], F32, name="rope")
         c_banks = {}
         r_bank = bank_tile([P, TOKEN_TILES, ROPE_DIM], F32, R_BANK)
-        k_out = []
-        for i in range(TOKEN_TILES):
-            k_tile = keep.tile(
-                [P, K_SLOTS, CHUNK_HEADS, HEAD_DIM + ROPE_DIM], F32, name="k_out%d" % i
-            )
-            k_out.append(k_tile)
 
         def transpose_x(i, copies):
             words = x_raw[i][:].bitcast(F32).rearrange("p (g q u) -> p g u q", g=A_PASSES, u=2)
@@ -275,39 +300,41 @@ def tile_mla_pb_kernel(tc, x, wkv_a, wkv_b, out_0, out_1):
                 in_=cn_grouped[:].rearrange("p w t -> p (w t)"),
             )
 
-        def multiply_rope_key():
+        def multiply_rope_key(tiles):
+            products = stage.tile([P, 2, 2 * PAIR, HALF], F32, name="products")
             nc.vector.tensor_tensor(
                 out=products[:],
-                in0=r_bank[:]
+                in0=r_bank[:, tiles, :]
                 .rearrange("p i (h j) -> p (i h) j", j=HALF)
                 .unsqueeze(1)
-                .to_broadcast([P, 2, 2 * TOKEN_TILES, HALF]),
-                in1=trig[:].unsqueeze(2).to_broadcast([P, 2, 2 * TOKEN_TILES, HALF]),
+                .to_broadcast([P, 2, 2 * PAIR, HALF]),
+                in1=trig[:].unsqueeze(2).to_broadcast([P, 2, 2 * PAIR, HALF]),
                 op=ALU.mult,
             )
+            return products
 
-        def rotate_rope_key():
+        def rotate_rope_key(tiles, products):
             by_half = products[:].rearrange("p f (i h) j -> p f i h j", h=2)
             nc.vector.tensor_tensor(
-                out=rope[:, :, 0, :],
+                out=rope[:, tiles, 0, :],
                 in0=by_half[:, 0, :, 0, :],
                 in1=by_half[:, 1, :, 1, :],
                 op=ALU.subtract,
             )
             nc.vector.tensor_tensor(
-                out=rope[:, :, 1, :],
+                out=rope[:, tiles, 1, :],
                 in0=by_half[:, 0, :, 1, :],
                 in1=by_half[:, 1, :, 0, :],
                 op=ALU.add,
             )
 
-        def repeat_rope_key(i, slot):
-            nc.vector.tensor_copy(
-                out=k_out[i][:, slot, :, HEAD_DIM : HEAD_DIM + ROPE_DIM],
+        def store_rope_key(i):
+            nc.sync.dma_start(
+                out=k_rows[i * P : (i + 1) * P, :, HEAD_DIM : HEAD_DIM + ROPE_DIM],
                 in_=rope[:, i, :, :]
                 .rearrange("p h j -> p (h j)")
                 .unsqueeze(1)
-                .to_broadcast([P, CHUNK_HEADS, ROPE_DIM]),
+                .to_broadcast([P, HEADS, ROPE_DIM]),
             )
 
         def regroup_b(kind, chunk):
@@ -343,16 +370,12 @@ def tile_mla_pb_kernel(tc, x, wkv_a, wkv_b, out_0, out_1):
             return u_bank
 
         def store(kind, chunk, i, u_bank, copy):
-            if kind == NOPE:
-                out_heads = k_out[i][:, chunk % K_SLOTS, :, :]
-                out_rows, width = k_rows, HEAD_DIM + ROPE_DIM
-            else:
-                v_out = outs.tile([P, CHUNK_HEADS, HEAD_DIM], F32, name="v_out")
-                out_heads, out_rows, width = v_out[:], v_rows, HEAD_DIM
-            copy(out=out_heads[:, :, 0:HEAD_DIM], in_=u_bank[:])
+            u_out = outs.tile([P, CHUNK_HEADS, HEAD_DIM], F32, name="u_out")
+            copy(out=u_out[:], in_=u_bank[:])
+            out_rows = (k_rows, v_rows)[kind]
             heads = slice(chunk * CHUNK_HEADS, (chunk + 1) * CHUNK_HEADS)
             nc.sync.dma_start(
-                out=out_rows[i * P : (i + 1) * P, heads, :], in_=out_heads[:, :, 0:width]
+                out=out_rows[i * P : (i + 1) * P, heads, 0:HEAD_DIM], in_=u_out[:]
             )
 
         V, A = nc.vector.tensor_copy, nc.scalar.copy
@@ -360,57 +383,63 @@ def tile_mla_pb_kernel(tc, x, wkv_a, wkv_b, out_0, out_1):
         x_grouped = transpose_x(0, (A, A))
         for n in range(TOKEN_TILES):
             last = n + 1 == TOKEN_TILES
+            for step in rope_steps[ROPE_STEPS_FIRST + 2 * n : ROPE_STEPS_FIRST + 2 * n + 1]:
+                step()
             quantise_a(n, a_grouped)
             for i in range(n):
                 c_pass(i, n)
             if not last:
                 a_grouped = regroup_a(n + 1)
+            for step in rope_steps[ROPE_STEPS_FIRST + 2 * n + 1 : ROPE_STEPS_FIRST + 2 * n + 2]:
+                step()
             quantise_x(n, x_grouped)
             if last:
-                multiply_r(range(n))
+                multiply_r(range(0, PAIR))
             else:
                 x_grouped = transpose_x(n + 1, (A, A))
             for g in range(n + 1):
                 c_pass(n, g)
-        multiply_r([TOKEN_TILES - 1])
+        multiply_r(range(PAIR, 2 * PAIR))
+        first, second = slice(0, PAIR), slice(PAIR, 2 * PAIR)
+        products = multiply_rope_key(first)
         bg = regroup_b(NOPE, 0)
+        rotate_rope_key(first, products)
+        store_rope_key(0)
+        store_rope_key(1)
+        nc.scalar.activation(out=warm_up[:, 1:2], in_=eps[:], func=ACT.Abs_reciprocal_sqrt)
         square_c(0)
         square_c(1)
-        norm_factors(slice(0, 2))
+        norm_factors(first)
         cn0 = scale_c(0)
         quantise_b(NOPE, 0, bg)
         cn1 = scale_c(1)
-        multiply_rope_key()
+        products = multiply_rope_key(second)
         cg0 = transpose_cn(0, cn0, V)
         cg1 = transpose_cn(1, cn1, V)
         quantise_cn(0, cg0)
         quantise_cn(1, cg1)
-        rotate_rope_key()
+        rotate_rope_key(second, products)
         square_c(2)
         square_c(3)
-        norm_factors(slice(2, 4))
+        norm_factors(second)
         u0 = multiply_b(NOPE, 0, 0, 5)
         u1 = multiply_b(NOPE, 0, 1, 6)
+        bg = regroup_b(NOPE, 1)
+        store_rope_key(2)
+        store_rope_key(3)
         cn2 = scale_c(2)
         cn3 = scale_c(3)
-        repeat_rope_key(0, 0)
         store(NOPE, 0, 0, u0, A)
         cg2 = transpose_cn(2, cn2, V)
-        repeat_rope_key(1, 0)
         store(NOPE, 0, 1, u1, A)
         cg3 = transpose_cn(3, cn3, V)
         quantise_cn(2, cg2)
         quantise_cn(3, cg3)
-        bg = regroup_b(NOPE, 1)
-        repeat_rope_key(2, 0)
         u = multiply_b(NOPE, 0, 2, 0)
         store(NOPE, 0, 2, u, A)
-        repeat_rope_key(3, 0)
         u = multiply_b(NOPE, 0, 3, 1)
         store(NOPE, 0, 3, u, A)
         quantise_b(NOPE, 1, bg)
-        for i in range(TOKEN_TILES):
-            repeat_rope_key(i, 1)
         number = 2
         items = [(NOPE, 1), (NOPE, 2), (NOPE, 3), (VALUE, 0), (VALUE, 1), (VALUE, 2), (VALUE, 3)]
         bg = regroup_b(*items[1])

@@ -24,8 +24,6 @@ A_PASSES = DIM // K_PASS
 LATENT = 512
 ROPE_DIM = 128
 HALF = ROPE_DIM // 2
-DOUBLINGS = 6
-assert 2**DOUBLINGS == HALF
 A_COLS = LATENT + ROPE_DIM
 HEADS = 16
 HEAD_DIM = 128
@@ -38,14 +36,14 @@ CHUNKS = HEADS // CHUNK_HEADS
 CHUNK_COLS = CHUNK_HEADS * 2 * HEAD_DIM
 NOPE = 0
 VALUE = 1
-A_VECTOR_COLS = 384
-ROPE_STEPS_FIRST = 8
+A_VECTOR_COLS = 400
+A_VECTOR_COLS_FIRST = 512
+COARSE = 8
+FINE = HALF // COARSE
 RUN = 4
-C_BANKS = (0, 1, 2, 3)
-X_BANKS = (4, 5)
-R_BANK = 6
-CN_BANKS = (7, 4)
-U_BUFS = 24
+PSUM_BANKS = 8
+V_BUFS = 6
+K_SLOTS = 2
 PAIR = 2
 
 FLOPS = 2 * TOKENS * DIM * A_COLS + 2 * TOKENS * LATENT * HEADS * 2 * HEAD_DIM
@@ -58,54 +56,68 @@ def regroup(copy, grouped, raw):
     )
 
 
-def rope_table_steps(nc, pool):
-    theta = pool.tile([P, HALF], F32, name="theta")
-    turns = pool.tile([P, 2, HALF], F32, name="turns")
-    whole_int = pool.tile([P, 2, HALF], I32, name="whole_int")
-    whole = pool.tile([P, 2, HALF], F32, name="whole")
-    left = pool.tile([P, 2, HALF], F32, name="left")
-    minus = pool.tile([P, 2, HALF], F32, name="minus")
-    trig = pool.tile([P, 2, HALF], F32, name="trig")
-    per_turn = POSITION / (2.0 * math.pi)
-
-    def double(width):
+def build_rotation(nc, pool, ident):
+    powers = pool.tile([P, COARSE + FINE], F32, name="powers")
+    one = pool.tile([P, 1], F32, name="one")
+    nc.vector.memset(one[:], 1.0)
+    exponents = [FINE * a for a in range(COARSE)] + list(range(FINE))
+    for n, exponent in enumerate(exponents):
         nc.vector.tensor_scalar(
-            out=theta[:, width : 2 * width],
-            in0=theta[:, 0:width],
-            scalar1=ROPE_BASE ** (-width / HALF),
+            out=powers[:, n : n + 1],
+            in0=one[:],
+            scalar1=ROPE_BASE ** (-exponent / HALF),
             scalar2=None,
             op0=ALU.mult,
         )
-
-    def to_turns():
-        nc.vector.tensor_scalar(
-            out=turns[:, 0, :], in0=theta[:], scalar1=per_turn, scalar2=0.25, op0=ALU.mult, op1=ALU.add
-        )
-        nc.vector.tensor_scalar(
-            out=turns[:, 1, :], in0=theta[:], scalar1=per_turn, scalar2=None, op0=ALU.mult
-        )
-
-    def take_off_whole_turns():
-        nc.vector.tensor_tensor(out=left[:], in0=turns[:], in1=whole[:], op=ALU.subtract)
-
-    def fold():
+    shift = pool.tile([P, 2, HALF], F32, name="shift")
+    per_turn = POSITION / (2.0 * math.pi)
+    for f, quarter in enumerate((0.25, 0.0)):
+        whole = [round(per_turn * ROPE_BASE ** (-j / HALF) + quarter) for j in range(HALF)]
+        for number in sorted(set(whole)):
+            begin = whole.index(number)
+            end = begin + whole.count(number)
+            nc.gpsimd.memset(shift[:, f, begin:end], quarter - number)
+    theta = pool.tile([P, COARSE, FINE], F32, name="theta")
+    nc.vector.tensor_tensor(
+        out=theta[:],
+        in0=powers[:, 0:COARSE].unsqueeze(2).to_broadcast([P, COARSE, FINE]),
+        in1=powers[:, COARSE : COARSE + FINE].unsqueeze(1).to_broadcast([P, COARSE, FINE]),
+        op=ALU.mult,
+    )
+    turns = pool.tile([P, 2, HALF], F32, name="turns")
+    for f in range(2):
         nc.vector.scalar_tensor_tensor(
-            out=minus[:], in0=left[:], scalar=0.5, in1=left[:], op0=ALU.is_gt, op1=ALU.subtract
+            out=turns[:, f, :],
+            in0=theta[:].rearrange("p a b -> p (a b)"),
+            scalar=per_turn,
+            in1=shift[:, f, :],
+            op0=ALU.mult,
+            op1=ALU.add,
         )
-
-    steps = [lambda: nc.vector.memset(theta[:, 0:1], 1.0)]
-    steps += [lambda width=2**n: double(width) for n in range(DOUBLINGS)]
-    steps += [
-        to_turns,
-        lambda: nc.vector.tensor_copy(out=whole_int[:], in_=turns[:]),
-        lambda: nc.vector.tensor_copy(out=whole[:], in_=whole_int[:]),
-        take_off_whole_turns,
-        fold,
-        lambda: nc.scalar.activation(
-            out=trig[:], in_=minus[:], func=ACT.Sin, scale=-2.0 * math.pi
-        ),
-    ]
-    return trig, steps
+    trig = pool.tile([P, 2, HALF], F32, name="trig")
+    nc.scalar.activation(out=trig[:], in_=turns[:], func=ACT.Sin, scale=2.0 * math.pi)
+    by_half = ident[:].rearrange("p (h j) -> p h j", h=2)
+    cosines = pool.tile([P, 2, HALF], F32, name="cosines")
+    nc.vector.tensor_tensor(
+        out=cosines[:],
+        in0=by_half,
+        in1=trig[:, 0, :].unsqueeze(1).to_broadcast([P, 2, HALF]),
+        op=ALU.mult,
+    )
+    sines = pool.tile([P, 2, HALF], F32, name="sines")
+    for h in range(2):
+        nc.vector.tensor_tensor(
+            out=sines[:, h, :], in0=by_half[:, 1 - h, :], in1=trig[:, 1, :], op=ALU.mult
+        )
+    rotation = pool.tile([P, ROPE_DIM], F32, name="rotation")
+    for h, op in enumerate((ALU.subtract, ALU.add)):
+        nc.vector.tensor_tensor(
+            out=rotation[:, h * HALF : (h + 1) * HALF],
+            in0=cosines[:, h, :],
+            in1=sines[:, h, :],
+            op=op,
+        )
+    return rotation
 
 
 def tile_mla_pb_kernel(tc, x, wkv_a, wkv_b, out_0, out_1):
@@ -119,8 +131,8 @@ def tile_mla_pb_kernel(tc, x, wkv_a, wkv_b, out_0, out_1):
         keep = stack.enter_context(tc.tile_pool(name="keep", bufs=1))
         stage = stack.enter_context(tc.tile_pool(name="stage", bufs=2))
         b_stage = stack.enter_context(tc.tile_pool(name="b_stage", bufs=2))
-        outs = stack.enter_context(tc.tile_pool(name="outs", bufs=U_BUFS))
-        psum = stack.enter_context(tc.psum_pool(name="psum", bufs=1))
+        outs = stack.enter_context(tc.tile_pool(name="outs", bufs=V_BUFS))
+        psum = stack.enter_context(tc.psum_pool(name="psum", bufs=PSUM_BANKS // 2))
 
         x_raw = [None] * TOKEN_TILES
         a_raw = [None] * A_PASSES
@@ -158,11 +170,10 @@ def tile_mla_pb_kernel(tc, x, wkv_a, wkv_b, out_0, out_1):
         make_identity(nc, ident_bf16[:])
         eps = keep.tile([P, 1], F32, name="eps")
         nc.vector.memset(eps[:], EPS)
-        trig, rope_steps = rope_table_steps(nc, keep)
-        for step in rope_steps[:ROPE_STEPS_FIRST]:
-            step()
         warm_up = keep.tile([P, 2], F32, name="warm_up")
         nc.scalar.activation(out=warm_up[:, 0:1], in_=eps[:], func=ACT.Sin)
+        rotation = build_rotation(nc, keep, ident_f32)
+        nc.scalar.activation(out=warm_up[:, 1:2], in_=eps[:], func=ACT.Abs_reciprocal_sqrt)
 
         x_codes = keep.tile([P, TOKEN_TILES, A_PASSES, P], U32, name="x_codes", align_bytes=64)
         x_scales = keep.tile([P, TOKEN_TILES, A_PASSES, P], U8, name="x_scales", align_bytes=64)
@@ -173,29 +184,40 @@ def tile_mla_pb_kernel(tc, x, wkv_a, wkv_b, out_0, out_1):
         b_codes = keep.tile([P, 2, HEADS, HEAD_DIM], U32, name="b_codes", align_bytes=64)
         b_scales = keep.tile([P, 2, HEADS, HEAD_DIM], U8, name="b_scales", align_bytes=64)
 
-        def bank_tile(shape, dtype, number):
-            bank = psum.tile(shape, dtype, name="bank%d" % number)
+        def bank_tile(shape, dtype, kind="any"):
+            bank = psum.tile(shape, dtype, name=kind + "_bank")
             return bank
 
         sum_squares = keep.tile([P, TOKEN_TILES], F32, name="sum_squares")
         inv_rms = keep.tile([P, TOKEN_TILES], F32, name="inv_rms")
-        rope = keep.tile([P, TOKEN_TILES, 2, HALF], F32, name="rope")
-        c_banks = {}
-        r_bank = bank_tile([P, TOKEN_TILES, ROPE_DIM], F32, R_BANK)
-
-        def transpose_x(i, copies):
-            words = x_raw[i][:].bitcast(F32).rearrange("p (g q u) -> p g u q", g=A_PASSES, u=2)
-            x_grouped = stage.tile([P, A_PASSES * P * PACK], BF16, name="x_grouped", align_bytes=64)
-            grouped_words = x_grouped[:].bitcast(F32).rearrange(
-                "p (g w u) -> p g w u", g=A_PASSES, u=2
+        rope = keep.tile([P, TOKEN_TILES, ROPE_DIM], F32, name="rope")
+        k_out = []
+        for i in range(TOKEN_TILES):
+            k_tile = keep.tile(
+                [P, K_SLOTS, CHUNK_HEADS, HEAD_DIM + ROPE_DIM], F32, name="k_out%d" % i
             )
-            for half, copy in enumerate(copies):
-                x_bank = bank_tile([P, 2, 2, P], F32, X_BANKS[half])
+            k_out.append(k_tile)
+        c_banks = {}
+
+        def transpose_x(i):
+            words = x_raw[i][:].bitcast(F32).rearrange("p (g q u) -> p g u q", g=A_PASSES, u=2)
+            banks = []
+            for half in range(2):
+                x_bank = bank_tile([P, 2, 2, P], F32)
                 for g in range(2):
                     for u in range(2):
                         nc.tensor.transpose(
                             x_bank[:, g, u, :], words[:, 2 * half + g, u, :], ident_f32[:]
                         )
+                banks.append(x_bank)
+            return banks
+
+        def empty_x(banks, copies):
+            x_grouped = stage.tile([P, A_PASSES * P * PACK], BF16, name="x_grouped", align_bytes=64)
+            grouped_words = x_grouped[:].bitcast(F32).rearrange(
+                "p (g w u) -> p g w u", g=A_PASSES, u=2
+            )
+            for half, (x_bank, copy) in enumerate(zip(banks, copies)):
                 copy(
                     out=grouped_words[:, 2 * half : 2 * half + 2, :, :],
                     in_=x_bank[:].rearrange("p g u w -> p g w u"),
@@ -211,16 +233,9 @@ def tile_mla_pb_kernel(tc, x, wkv_a, wkv_b, out_0, out_1):
 
         def regroup_a(g):
             a_grouped = stage.tile([P, A_COLS, PACK], BF16, name="a_grouped", align_bytes=64)
-            regroup(
-                nc.vector.tensor_copy,
-                a_grouped[:, 0:A_VECTOR_COLS, :],
-                a_raw[g][:, :, 0:A_VECTOR_COLS],
-            )
-            regroup(
-                nc.scalar.copy,
-                a_grouped[:, A_VECTOR_COLS:A_COLS, :],
-                a_raw[g][:, :, A_VECTOR_COLS:A_COLS],
-            )
+            split = A_VECTOR_COLS_FIRST if g in (0, 3) else A_VECTOR_COLS
+            regroup(nc.vector.tensor_copy, a_grouped[:, 0:split, :], a_raw[g][:, :, 0:split])
+            regroup(nc.scalar.copy, a_grouped[:, split:A_COLS, :], a_raw[g][:, :, split:A_COLS])
             return a_grouped
 
         def quantise_a(g, a_grouped):
@@ -233,7 +248,7 @@ def tile_mla_pb_kernel(tc, x, wkv_a, wkv_b, out_0, out_1):
 
         def c_pass(i, g):
             if g == 0:
-                c_banks[i] = bank_tile([P, LATENT], F32, C_BANKS[i])
+                c_banks[i] = bank_tile([P, LATENT], F32, "c")
             nc.tensor.matmul_mx(
                 out=c_banks[i][:],
                 lhsT=x_codes[:, i, g, :].bitcast(FP8X4),
@@ -245,17 +260,19 @@ def tile_mla_pb_kernel(tc, x, wkv_a, wkv_b, out_0, out_1):
             )
 
         def multiply_r(tiles):
-            for i in tiles:
+            r_bank = bank_tile([P, PAIR, P], F32)
+            for n, i in enumerate(tiles):
                 for g in range(A_PASSES):
                     nc.tensor.matmul_mx(
-                        out=r_bank[:, i, :],
-                        lhsT=x_codes[:, i, g, :].bitcast(FP8X4),
-                        lhsT_scale=x_scales[:, i, g, :],
-                        rhs=a_codes[:, g, LATENT:A_COLS].bitcast(FP8X4),
-                        rhs_scale=a_scales[:, g, LATENT:A_COLS],
+                        out=r_bank[:, n, :],
+                        lhsT=a_codes[:, g, LATENT:A_COLS].bitcast(FP8X4),
+                        lhsT_scale=a_scales[:, g, LATENT:A_COLS],
+                        rhs=x_codes[:, i, g, :].bitcast(FP8X4),
+                        rhs_scale=x_scales[:, i, g, :],
                         start=(g == 0),
                         stop=(g == A_PASSES - 1),
                     )
+            return r_bank
 
         def square_c(i):
             squares = stage.tile([P, LATENT], F32, name="squares")
@@ -285,10 +302,13 @@ def tile_mla_pb_kernel(tc, x, wkv_a, wkv_b, out_0, out_1):
             )
             return cn
 
-        def transpose_cn(i, cn, copy):
-            cn_bank = bank_tile([P, PACK, P], BF16, CN_BANKS[i % 2])
+        def transpose_cn(cn):
+            cn_bank = bank_tile([P, PACK, P], BF16)
             for t in range(PACK):
                 nc.tensor.transpose(cn_bank[:, t, :], cn[:, t, :], ident_bf16[:])
+            return cn_bank
+
+        def empty_cn(cn_bank, copy):
             cn_grouped = stage.tile([P, P, PACK], BF16, name="cn_grouped", align_bytes=64)
             copy(out=cn_grouped[:], in_=cn_bank[:].rearrange("p t w -> p w t"))
             return cn_grouped
@@ -300,41 +320,28 @@ def tile_mla_pb_kernel(tc, x, wkv_a, wkv_b, out_0, out_1):
                 in_=cn_grouped[:].rearrange("p w t -> p (w t)"),
             )
 
-        def multiply_rope_key(tiles):
-            products = stage.tile([P, 2, 2 * PAIR, HALF], F32, name="products")
-            nc.vector.tensor_tensor(
-                out=products[:],
-                in0=r_bank[:, tiles, :]
-                .rearrange("p i (h j) -> p (i h) j", j=HALF)
-                .unsqueeze(1)
-                .to_broadcast([P, 2, 2 * PAIR, HALF]),
-                in1=trig[:].unsqueeze(2).to_broadcast([P, 2, 2 * PAIR, HALF]),
-                op=ALU.mult,
-            )
-            return products
+        def empty_r(r_bank, copy):
+            r_transposed = stage.tile([P, PAIR, P], F32, name="r_transposed")
+            copy(out=r_transposed[:], in_=r_bank[:])
+            return r_transposed
 
-        def rotate_rope_key(tiles, products):
-            by_half = products[:].rearrange("p f (i h) j -> p f i h j", h=2)
-            nc.vector.tensor_tensor(
-                out=rope[:, tiles, 0, :],
-                in0=by_half[:, 0, :, 0, :],
-                in1=by_half[:, 1, :, 1, :],
-                op=ALU.subtract,
-            )
-            nc.vector.tensor_tensor(
-                out=rope[:, tiles, 1, :],
-                in0=by_half[:, 0, :, 1, :],
-                in1=by_half[:, 1, :, 0, :],
-                op=ALU.add,
-            )
+        def rotate_rope_key(r_transposed):
+            rope_bank = bank_tile([P, PAIR, ROPE_DIM], F32)
+            for n in range(PAIR):
+                nc.tensor.matmul(
+                    rope_bank[:, n, :], lhsT=r_transposed[:, n, :], rhs=rotation[:], start=True, stop=True
+                )
+            return rope_bank
 
-        def store_rope_key(i):
-            nc.sync.dma_start(
-                out=k_rows[i * P : (i + 1) * P, :, HEAD_DIM : HEAD_DIM + ROPE_DIM],
-                in_=rope[:, i, :, :]
-                .rearrange("p h j -> p (h j)")
+        def empty_rope_key(tiles, rope_bank, copy):
+            copy(out=rope[:, tiles, :], in_=rope_bank[:])
+
+        def repeat_rope_key(i, slot):
+            nc.vector.tensor_copy(
+                out=k_out[i][:, slot, :, HEAD_DIM : HEAD_DIM + ROPE_DIM],
+                in_=rope[:, i, :]
                 .unsqueeze(1)
-                .to_broadcast([P, HEADS, ROPE_DIM]),
+                .to_broadcast([P, CHUNK_HEADS, ROPE_DIM]),
             )
 
         def regroup_b(kind, chunk):
@@ -355,8 +362,8 @@ def tile_mla_pb_kernel(tc, x, wkv_a, wkv_b, out_0, out_1):
                 in_=b_grouped[:].rearrange("p c t -> p (c t)"),
             )
 
-        def multiply_b(kind, chunk, i, number):
-            u_bank = bank_tile([P, CHUNK_HEADS, HEAD_DIM], F32, number)
+        def multiply_b(kind, chunk, i, bank="any"):
+            u_bank = bank_tile([P, CHUNK_HEADS, HEAD_DIM], F32, bank)
             for h in range(CHUNK_HEADS):
                 nc.tensor.matmul_mx(
                     out=u_bank[:, h, :],
@@ -369,86 +376,133 @@ def tile_mla_pb_kernel(tc, x, wkv_a, wkv_b, out_0, out_1):
                 )
             return u_bank
 
-        def store(kind, chunk, i, u_bank, copy):
-            u_out = outs.tile([P, CHUNK_HEADS, HEAD_DIM], F32, name="u_out")
-            copy(out=u_out[:], in_=u_bank[:])
-            out_rows = (k_rows, v_rows)[kind]
-            heads = slice(chunk * CHUNK_HEADS, (chunk + 1) * CHUNK_HEADS)
+        def empty_k(chunk, i, u_bank, copy):
+            copy(out=k_out[i][:, chunk % K_SLOTS, :, 0:HEAD_DIM], in_=u_bank[:])
+
+        def store_k(first, count, i):
+            slot = first % K_SLOTS
             nc.sync.dma_start(
-                out=out_rows[i * P : (i + 1) * P, heads, 0:HEAD_DIM], in_=u_out[:]
+                out=k_rows[i * P : (i + 1) * P, first * CHUNK_HEADS : (first + count) * CHUNK_HEADS, :],
+                in_=k_out[i][:, slot : slot + count, :, :].rearrange("p s h d -> p (s h) d"),
+            )
+
+        def multiply_and_store_v(first, count, i, copies):
+            v_out = outs.tile([P, count, CHUNK_HEADS, HEAD_DIM], F32, name="v_out")
+            for n in range(count):
+                u_bank = multiply_b(VALUE, first + n, i, ("any", "c")[n])
+                copies[n](out=v_out[:, n, :, :], in_=u_bank[:])
+            nc.sync.dma_start(
+                out=v_rows[i * P : (i + 1) * P, first * CHUNK_HEADS : (first + count) * CHUNK_HEADS, :],
+                in_=v_out[:].rearrange("p s h d -> p (s h) d"),
             )
 
         V, A = nc.vector.tensor_copy, nc.scalar.copy
-        a_grouped = regroup_a(0)
-        x_grouped = transpose_x(0, (A, A))
-        for n in range(TOKEN_TILES):
-            last = n + 1 == TOKEN_TILES
-            for step in rope_steps[ROPE_STEPS_FIRST + 2 * n : ROPE_STEPS_FIRST + 2 * n + 1]:
-                step()
-            quantise_a(n, a_grouped)
+        first, second = slice(0, PAIR), slice(PAIR, 2 * PAIR)
+        ag = regroup_a(0)
+        xb = transpose_x(0)
+        xg = empty_x(xb, (A, A))
+        for n in range(TOKEN_TILES - 1):
+            quantise_a(n, ag)
             for i in range(n):
                 c_pass(i, n)
-            if not last:
-                a_grouped = regroup_a(n + 1)
-            for step in rope_steps[ROPE_STEPS_FIRST + 2 * n + 1 : ROPE_STEPS_FIRST + 2 * n + 2]:
-                step()
-            quantise_x(n, x_grouped)
-            if last:
-                multiply_r(range(0, PAIR))
+            ag = regroup_a(n + 1)
+            if n + 1 < TOKEN_TILES - 1:
+                quantise_x(n, xg)
             else:
-                x_grouped = transpose_x(n + 1, (A, A))
-            for g in range(n + 1):
-                c_pass(n, g)
-        multiply_r(range(PAIR, 2 * PAIR))
-        first, second = slice(0, PAIR), slice(PAIR, 2 * PAIR)
-        products = multiply_rope_key(first)
-        bg = regroup_b(NOPE, 0)
-        rotate_rope_key(first, products)
-        store_rope_key(0)
-        store_rope_key(1)
-        nc.scalar.activation(out=warm_up[:, 1:2], in_=eps[:], func=ACT.Abs_reciprocal_sqrt)
+                xg2 = xg
+            xb = transpose_x(n + 1)
+            xg = empty_x(xb, (A, A))
+            if n + 1 < TOKEN_TILES - 1:
+                for g in range(n + 1):
+                    c_pass(n, g)
+        quantise_a(3, ag)
+        c_pass(0, 3)
+        c_pass(1, 3)
+        r0 = multiply_r(range(0, PAIR))
+        quantise_x(2, xg2)
+        for g in range(A_PASSES):
+            c_pass(2, g)
+        quantise_x(3, xg)
         square_c(0)
+        rt = empty_r(r0, A)
         square_c(1)
         norm_factors(first)
+        bg = regroup_b(NOPE, 0)
+        rope_bank = rotate_rope_key(rt)
+        c_pass(3, 0)
+        c_pass(3, 1)
         cn0 = scale_c(0)
+        empty_rope_key(first, rope_bank, A)
+        t0 = transpose_cn(cn0)
+        c_pass(3, 2)
+        c_pass(3, 3)
         quantise_b(NOPE, 0, bg)
         cn1 = scale_c(1)
-        products = multiply_rope_key(second)
-        cg0 = transpose_cn(0, cn0, V)
-        cg1 = transpose_cn(1, cn1, V)
+        cg0 = empty_cn(t0, V)
+        repeat_rope_key(0, 0)
+        t1 = transpose_cn(cn1)
         quantise_cn(0, cg0)
-        quantise_cn(1, cg1)
-        rotate_rope_key(second, products)
         square_c(2)
+        u0 = multiply_b(NOPE, 0, 0)
+        cg1 = empty_cn(t1, V)
+        repeat_rope_key(1, 0)
+        quantise_cn(1, cg1)
         square_c(3)
-        norm_factors(second)
-        u0 = multiply_b(NOPE, 0, 0, 5)
-        u1 = multiply_b(NOPE, 0, 1, 6)
+        empty_k(0, 0, u0, A)
+        store_k(0, 1, 0)
+        r1 = multiply_r(range(PAIR, 2 * PAIR))
+        u1 = multiply_b(NOPE, 0, 1)
         bg = regroup_b(NOPE, 1)
-        store_rope_key(2)
-        store_rope_key(3)
+        norm_factors(second)
+        rt = empty_r(r1, A)
         cn2 = scale_c(2)
-        cn3 = scale_c(3)
-        store(NOPE, 0, 0, u0, A)
-        cg2 = transpose_cn(2, cn2, V)
-        store(NOPE, 0, 1, u1, A)
-        cg3 = transpose_cn(3, cn3, V)
-        quantise_cn(2, cg2)
-        quantise_cn(3, cg3)
-        u = multiply_b(NOPE, 0, 2, 0)
-        store(NOPE, 0, 2, u, A)
-        u = multiply_b(NOPE, 0, 3, 1)
-        store(NOPE, 0, 3, u, A)
+        empty_k(0, 1, u1, A)
+        store_k(0, 1, 1)
+        t2 = transpose_cn(cn2)
+        rope_bank = rotate_rope_key(rt)
+        repeat_rope_key(0, 1)
         quantise_b(NOPE, 1, bg)
-        number = 2
-        items = [(NOPE, 1), (NOPE, 2), (NOPE, 3), (VALUE, 0), (VALUE, 1), (VALUE, 2), (VALUE, 3)]
-        bg = regroup_b(*items[1])
-        for k, (kind, chunk) in enumerate(items):
+        cn3 = scale_c(3)
+        cg2 = empty_cn(t2, V)
+        u0 = multiply_b(NOPE, 1, 0, "c")
+        u1 = multiply_b(NOPE, 1, 1, "c")
+        t3 = transpose_cn(cn3)
+        empty_rope_key(second, rope_bank, A)
+        repeat_rope_key(1, 1)
+        quantise_cn(2, cg2)
+        empty_k(1, 0, u0, A)
+        store_k(1, 1, 0)
+        cg3 = empty_cn(t3, V)
+        empty_k(1, 1, u1, A)
+        store_k(1, 1, 1)
+        u2 = multiply_b(NOPE, 0, 2)
+        repeat_rope_key(2, 0)
+        quantise_cn(3, cg3)
+        empty_k(0, 2, u2, A)
+        store_k(0, 1, 2)
+        u3 = multiply_b(NOPE, 0, 3)
+        repeat_rope_key(3, 0)
+        empty_k(0, 3, u3, A)
+        store_k(0, 1, 3)
+        bg = regroup_b(NOPE, 2)
+        for i in range(PAIR, TOKEN_TILES):
+            repeat_rope_key(i, 1)
+            u = multiply_b(NOPE, 1, i, "c")
+            empty_k(1, i, u, A)
+            store_k(1, 1, i)
+        bh = regroup_b(NOPE, 3)
+        quantise_b(NOPE, 2, bg)
+        quantise_b(NOPE, 3, bh)
+        for i in range(TOKEN_TILES):
+            for chunk in (2, 3):
+                u = multiply_b(NOPE, chunk, i, ("any", "c")[chunk - 2])
+                empty_k(chunk, i, u, A)
+            store_k(2, 2, i)
+        for chunk in (0, 2):
+            bg = regroup_b(VALUE, chunk)
+            bh = regroup_b(VALUE, chunk + 1)
+            quantise_b(VALUE, chunk, bg)
+            quantise_b(VALUE, chunk + 1, bh)
+        for chunk in (0, 2):
             for i in range(TOKEN_TILES):
-                u = multiply_b(kind, chunk, i, number % 8)
-                store(kind, chunk, i, u, A)
-                number += 1
-                if i == 0 and k + 1 < len(items):
-                    quantise_b(*items[k + 1], bg)
-                if i == 0 and k + 2 < len(items):
-                    bg = regroup_b(*items[k + 2])
+                multiply_and_store_v(chunk, 2, i, (A, V))

@@ -42,7 +42,7 @@ COARSE = 8
 FINE = HALF // COARSE
 RUN = 4
 PSUM_BANKS = 8
-V_BUFS = 6
+V_BUFS = 4
 K_SLOTS = 2
 PAIR = 2
 
@@ -149,20 +149,24 @@ def tile_mla_pb_kernel(tc, x, wkv_a, wkv_b, out_0, out_1):
             nc.sync.dma_start(out=raw[:], in_=rows.rearrange("(p t) c -> p t c", t=PACK))
             a_raw[g] = raw
 
-        def load_b(chunk):
-            raw = keep.tile([P, PACK, CHUNK_HEADS, 2, HEAD_DIM], BF16, name="b_raw%d" % chunk)
-            cols = wkv_b[:, chunk * CHUNK_COLS : (chunk + 1) * CHUNK_COLS]
+        def load_b(first, count):
+            raw = keep.tile(
+                [P, PACK, count * CHUNK_HEADS, 2, HEAD_DIM], BF16, name="b_raw%d" % first
+            )
+            cols = wkv_b[:, first * CHUNK_COLS : (first + count) * CHUNK_COLS]
             nc.sync.dma_start(
                 out=raw[:].rearrange("p t h f d -> p t (h f d)"),
                 in_=cols.rearrange("(p t) c -> p t c", t=PACK),
             )
-            b_raw[chunk] = raw
+            for n in range(count):
+                b_raw[first + n] = raw[:, :, n * CHUNK_HEADS : (n + 1) * CHUNK_HEADS, :, :]
 
         for n in range(TOKEN_TILES):
             load_a(n)
             load_x(n)
-        for chunk in range(CHUNKS):
-            load_b(chunk)
+        load_b(0, 1)
+        load_b(1, 1)
+        load_b(2, 2)
 
         ident_f32 = keep.tile([P, P], F32, name="ident_f32")
         make_identity(nc, ident_f32[:])
@@ -389,8 +393,8 @@ def tile_mla_pb_kernel(tc, x, wkv_a, wkv_b, out_0, out_1):
         def multiply_and_store_v(first, count, i, copies):
             v_out = outs.tile([P, count, CHUNK_HEADS, HEAD_DIM], F32, name="v_out")
             for n in range(count):
-                u_bank = multiply_b(VALUE, first + n, i, ("any", "c")[n])
-                copies[n](out=v_out[:, n, :, :], in_=u_bank[:])
+                u_bank = multiply_b(VALUE, first + n, i, ("any", "c")[n % 2])
+                copies[n % 2](out=v_out[:, n, :, :], in_=u_bank[:])
             nc.sync.dma_start(
                 out=v_rows[i * P : (i + 1) * P, first * CHUNK_HEADS : (first + count) * CHUNK_HEADS, :],
                 in_=v_out[:].rearrange("p s h d -> p (s h) d"),
@@ -503,6 +507,5 @@ def tile_mla_pb_kernel(tc, x, wkv_a, wkv_b, out_0, out_1):
             bh = regroup_b(VALUE, chunk + 1)
             quantise_b(VALUE, chunk, bg)
             quantise_b(VALUE, chunk + 1, bh)
-        for chunk in (0, 2):
-            for i in range(TOKEN_TILES):
-                multiply_and_store_v(chunk, 2, i, (A, V))
+        for i in range(TOKEN_TILES):
+            multiply_and_store_v(0, CHUNKS, i, (A, V))

@@ -161,10 +161,15 @@ def tile_mla_pb_kernel(tc, x, wkv_a, wkv_b, out_0, out_1):
             for n in range(count):
                 b_raw[first + n] = raw[:, :, n * CHUNK_HEADS : (n + 1) * CHUNK_HEADS, :, :]
 
-        for n in range(TOKEN_TILES):
-            load_a(n)
-            load_x(n)
+        load_a(0)
+        load_x(0)
+        load_a(1)
+        load_x(1)
+        load_a(2)
+        load_a(3)
+        load_x(2)
         load_b(0, 1)
+        load_x(3)
         load_b(1, 1)
         load_b(2, 2)
 
@@ -237,7 +242,7 @@ def tile_mla_pb_kernel(tc, x, wkv_a, wkv_b, out_0, out_1):
 
         def regroup_a(g):
             a_grouped = stage.tile([P, A_COLS, PACK], BF16, name="a_grouped", align_bytes=64)
-            split = A_VECTOR_COLS_FIRST if g in (0, 3) else A_VECTOR_COLS
+            split = A_VECTOR_COLS_FIRST if g == 0 else A_VECTOR_COLS
             regroup(nc.vector.tensor_copy, a_grouped[:, 0:split, :], a_raw[g][:, :, 0:split])
             regroup(nc.scalar.copy, a_grouped[:, split:A_COLS, :], a_raw[g][:, :, split:A_COLS])
             return a_grouped
@@ -264,7 +269,7 @@ def tile_mla_pb_kernel(tc, x, wkv_a, wkv_b, out_0, out_1):
             )
 
         def multiply_r(tiles):
-            r_bank = bank_tile([P, PAIR, P], F32)
+            r_bank = bank_tile([P, len(tiles), P], F32)
             for n, i in enumerate(tiles):
                 for g in range(A_PASSES):
                     nc.tensor.matmul_mx(
@@ -324,21 +329,21 @@ def tile_mla_pb_kernel(tc, x, wkv_a, wkv_b, out_0, out_1):
                 in_=cn_grouped[:].rearrange("p w t -> p (w t)"),
             )
 
-        def empty_r(r_bank, copy):
-            r_transposed = stage.tile([P, PAIR, P], F32, name="r_transposed")
+        def empty_r(tiles, r_bank, copy):
+            r_transposed = stage.tile([P, len(tiles), P], F32, name="r_transposed")
             copy(out=r_transposed[:], in_=r_bank[:])
             return r_transposed
 
-        def rotate_rope_key(r_transposed):
-            rope_bank = bank_tile([P, PAIR, ROPE_DIM], F32)
-            for n in range(PAIR):
+        def rotate_rope_key(tiles, r_transposed):
+            rope_bank = bank_tile([P, len(tiles), ROPE_DIM], F32)
+            for n in range(len(tiles)):
                 nc.tensor.matmul(
                     rope_bank[:, n, :], lhsT=r_transposed[:, n, :], rhs=rotation[:], start=True, stop=True
                 )
             return rope_bank
 
         def empty_rope_key(tiles, rope_bank, copy):
-            copy(out=rope[:, tiles, :], in_=rope_bank[:])
+            copy(out=rope[:, tiles.start : tiles.stop, :], in_=rope_bank[:])
 
         def repeat_rope_key(i, slot):
             nc.vector.tensor_copy(
@@ -402,106 +407,126 @@ def tile_mla_pb_kernel(tc, x, wkv_a, wkv_b, out_0, out_1):
 
         V, A = nc.vector.tensor_copy, nc.scalar.copy
         first, second = slice(0, PAIR), slice(PAIR, 2 * PAIR)
-        ag = regroup_a(0)
-        xb = transpose_x(0)
-        xg = empty_x(xb, (A, A))
-        for n in range(TOKEN_TILES - 1):
-            quantise_a(n, ag)
-            for i in range(n):
-                c_pass(i, n)
-            ag = regroup_a(n + 1)
-            if n + 1 < TOKEN_TILES - 1:
-                quantise_x(n, xg)
-            else:
-                xg2 = xg
-            xb = transpose_x(n + 1)
-            xg = empty_x(xb, (A, A))
-            if n + 1 < TOKEN_TILES - 1:
-                for g in range(n + 1):
-                    c_pass(n, g)
-        quantise_a(3, ag)
+        ag0 = regroup_a(0)
+        x0 = transpose_x(0)
+        xg0 = empty_x(x0, (A, A))
+        quantise_a(0, ag0)
+        ag1 = regroup_a(1)
+        quantise_x(0, xg0)
+        x1 = transpose_x(1)
+        c_pass(0, 0)
+        xg1 = empty_x(x1, (A, A))
+        quantise_a(1, ag1)
+        c_pass(0, 1)
+        ag2 = regroup_a(2)
+        quantise_x(1, xg1)
+        c_pass(1, 0)
+        c_pass(1, 1)
+        ag3 = regroup_a(3)
+        x2 = transpose_x(2)
+        quantise_a(2, ag2)
+        c_pass(0, 2)
+        xg2 = empty_x(x2, (A, A))
+        quantise_a(3, ag3)
         c_pass(0, 3)
+        c_pass(1, 2)
         c_pass(1, 3)
-        r0 = multiply_r(range(0, PAIR))
         quantise_x(2, xg2)
+        tiles = range(0, 2)
+        r_bank = multiply_r(tiles)
+        square_c(0)
+        bg = regroup_b(NOPE, 0)
         for g in range(A_PASSES):
             c_pass(2, g)
-        quantise_x(3, xg)
-        square_c(0)
-        rt = empty_r(r0, A)
         square_c(1)
+        rt = empty_r(tiles, r_bank, A)
         norm_factors(first)
-        bg = regroup_b(NOPE, 0)
-        rope_bank = rotate_rope_key(rt)
-        c_pass(3, 0)
-        c_pass(3, 1)
+        rope_bank = rotate_rope_key(tiles, rt)
         cn0 = scale_c(0)
-        empty_rope_key(first, rope_bank, A)
         t0 = transpose_cn(cn0)
-        c_pass(3, 2)
-        c_pass(3, 3)
         quantise_b(NOPE, 0, bg)
         cn1 = scale_c(1)
         cg0 = empty_cn(t0, V)
-        repeat_rope_key(0, 0)
         t1 = transpose_cn(cn1)
-        quantise_cn(0, cg0)
-        square_c(2)
-        u0 = multiply_b(NOPE, 0, 0)
+        empty_rope_key(tiles, rope_bank, A)
         cg1 = empty_cn(t1, V)
-        repeat_rope_key(1, 0)
+        square_c(2)
+        tiles = range(2, 3)
+        r_bank = multiply_r(tiles)
+        quantise_cn(0, cg0)
+        rt = empty_r(tiles, r_bank, A)
         quantise_cn(1, cg1)
-        square_c(3)
+        u0 = multiply_b(NOPE, 0, 0, "c")
+        u1 = multiply_b(NOPE, 0, 1, "c")
+        repeat_rope_key(0, 0)
+        rope_bank = rotate_rope_key(tiles, rt)
+        x3 = transpose_x(3)
+        bg = regroup_b(NOPE, 1)
+        norm_factors(slice(2, 3))
         empty_k(0, 0, u0, A)
         store_k(0, 1, 0)
-        r1 = multiply_r(range(PAIR, 2 * PAIR))
-        u1 = multiply_b(NOPE, 0, 1)
-        bg = regroup_b(NOPE, 1)
-        norm_factors(second)
-        rt = empty_r(r1, A)
         cn2 = scale_c(2)
+        repeat_rope_key(1, 0)
         empty_k(0, 1, u1, A)
         store_k(0, 1, 1)
         t2 = transpose_cn(cn2)
-        rope_bank = rotate_rope_key(rt)
-        repeat_rope_key(0, 1)
+        empty_rope_key(tiles, rope_bank, A)
+        xg3 = empty_x(x3, (A, A))
         quantise_b(NOPE, 1, bg)
-        cn3 = scale_c(3)
         cg2 = empty_cn(t2, V)
         u0 = multiply_b(NOPE, 1, 0, "c")
+        repeat_rope_key(0, 1)
         u1 = multiply_b(NOPE, 1, 1, "c")
-        t3 = transpose_cn(cn3)
-        empty_rope_key(second, rope_bank, A)
-        repeat_rope_key(1, 1)
         quantise_cn(2, cg2)
+        quantise_x(3, xg3)
+        u2 = multiply_b(NOPE, 0, 2)
+        u4 = multiply_b(NOPE, 1, 2)
+        for g in range(A_PASSES):
+            c_pass(3, g)
+        tiles = range(3, 4)
+        r_bank = multiply_r(tiles)
         empty_k(1, 0, u0, A)
         store_k(1, 1, 0)
-        cg3 = empty_cn(t3, V)
+        repeat_rope_key(1, 1)
         empty_k(1, 1, u1, A)
         store_k(1, 1, 1)
-        u2 = multiply_b(NOPE, 0, 2)
         repeat_rope_key(2, 0)
-        quantise_cn(3, cg3)
         empty_k(0, 2, u2, A)
         store_k(0, 1, 2)
-        u3 = multiply_b(NOPE, 0, 3)
+        repeat_rope_key(2, 1)
+        empty_k(1, 2, u4, A)
+        store_k(1, 1, 2)
+        square_c(3)
+        rt = empty_r(tiles, r_bank, A)
+        norm_factors(slice(3, 4))
+        bg = regroup_b(NOPE, 2)
+        cn3 = scale_c(3)
+        rope_bank = rotate_rope_key(tiles, rt)
+        t3 = transpose_cn(cn3)
+        empty_rope_key(tiles, rope_bank, A)
+        quantise_b(NOPE, 2, bg)
+        for i in range(PAIR):
+            u = multiply_b(NOPE, 2, i, "c")
+            empty_k(2, i, u, A)
+            store_k(2, 1, i)
+        cg3 = empty_cn(t3, V)
         repeat_rope_key(3, 0)
+        quantise_cn(3, cg3)
+        bg = regroup_b(NOPE, 3)
+        u3 = multiply_b(NOPE, 0, 3)
         empty_k(0, 3, u3, A)
         store_k(0, 1, 3)
-        bg = regroup_b(NOPE, 2)
-        for i in range(PAIR, TOKEN_TILES):
-            repeat_rope_key(i, 1)
-            u = multiply_b(NOPE, 1, i, "c")
-            empty_k(1, i, u, A)
-            store_k(1, 1, i)
-        bh = regroup_b(NOPE, 3)
-        quantise_b(NOPE, 2, bg)
-        quantise_b(NOPE, 3, bh)
+        u3 = multiply_b(NOPE, 1, 3, "c")
+        repeat_rope_key(3, 1)
+        empty_k(1, 3, u3, A)
+        store_k(1, 1, 3)
+        quantise_b(NOPE, 3, bg)
         for i in range(TOKEN_TILES):
-            for chunk in (2, 3):
+            rest = range(3, 4) if i < PAIR else range(2, 4)
+            for chunk in rest:
                 u = multiply_b(NOPE, chunk, i, ("any", "c")[chunk - 2])
                 empty_k(chunk, i, u, A)
-            store_k(2, 2, i)
+            store_k(rest.start, len(rest), i)
         for chunk in (0, 2):
             bg = regroup_b(VALUE, chunk)
             bh = regroup_b(VALUE, chunk + 1)

@@ -177,12 +177,21 @@ def tile_mla_pb_kernel(tc, x, wkv_a, wkv_b, out_0, out_1):
         make_identity(nc, ident_f32[:])
         ident_bf16 = keep.tile([P, P], BF16, name="ident_bf16")
         make_identity(nc, ident_bf16[:])
+        zeros = keep.tile([P, LATENT], BF16, name="zeros")
+        nc.vector.memset(zeros[:], 0.0)
         eps = keep.tile([P, 1], F32, name="eps")
         nc.vector.memset(eps[:], EPS)
         warm_up = keep.tile([P, 2], F32, name="warm_up")
         nc.scalar.activation(out=warm_up[:, 0:1], in_=eps[:], func=ACT.Sin)
         rotation = build_rotation(nc, keep, ident_f32)
         nc.scalar.activation(out=warm_up[:, 1:2], in_=eps[:], func=ACT.Abs_reciprocal_sqrt)
+
+        def warm_tensor(count):
+            idle_bank = psum.tile([P, LATENT], F32, name="any_bank")
+            for n in range(count):
+                nc.tensor.matmul(
+                    idle_bank[:], lhsT=zeros[:, 0:P], rhs=zeros[:], start=True, stop=True
+                )
 
         x_codes = keep.tile([P, TOKEN_TILES, A_PASSES, P], U32, name="x_codes", align_bytes=64)
         x_scales = keep.tile([P, TOKEN_TILES, A_PASSES, P], U8, name="x_scales", align_bytes=64)
@@ -407,17 +416,20 @@ def tile_mla_pb_kernel(tc, x, wkv_a, wkv_b, out_0, out_1):
 
         V, A = nc.vector.tensor_copy, nc.scalar.copy
         first, second = slice(0, PAIR), slice(PAIR, 2 * PAIR)
+        warm_tensor(10)
         ag0 = regroup_a(0)
         x0 = transpose_x(0)
         xg0 = empty_x(x0, (A, A))
         quantise_a(0, ag0)
         ag1 = regroup_a(1)
         quantise_x(0, xg0)
+        warm_tensor(3)
         x1 = transpose_x(1)
         c_pass(0, 0)
         xg1 = empty_x(x1, (A, A))
         quantise_a(1, ag1)
         c_pass(0, 1)
+        warm_tensor(2)
         ag2 = regroup_a(2)
         quantise_x(1, xg1)
         c_pass(1, 0)

@@ -42,7 +42,7 @@ COARSE = 8
 FINE = HALF // COARSE
 RUN = 4
 PSUM_BANKS = 8
-V_BUFS = 4
+V_BUFS = 8
 K_SLOTS = 2
 PAIR = 2
 
@@ -169,8 +169,8 @@ def tile_mla_pb_kernel(tc, x, wkv_a, wkv_b, out_0, out_1):
         load_a(3)
         load_x(2)
         load_b(0, 1)
-        load_x(3)
         load_b(1, 1)
+        load_x(3)
         load_b(2, 2)
 
         ident_f32 = keep.tile([P, P], F32, name="ident_f32")
@@ -256,13 +256,12 @@ def tile_mla_pb_kernel(tc, x, wkv_a, wkv_b, out_0, out_1):
             regroup(nc.scalar.copy, a_grouped[:, split:A_COLS, :], a_raw[g][:, :, split:A_COLS])
             return a_grouped
 
-        def quantise_a(g, a_grouped):
-            for first, last in ((0, LATENT), (LATENT, A_COLS)):
-                nc.vector.quantize_mx(
-                    out=a_codes[:, g, first:last].bitcast(FP8X4),
-                    scales=a_scales[:, g, first:last],
-                    in_=a_grouped[:, first:last, :].rearrange("p c t -> p (c t)"),
-                )
+        def quantise_a(g, a_grouped, first, last):
+            nc.vector.quantize_mx(
+                out=a_codes[:, g, first:last].bitcast(FP8X4),
+                scales=a_scales[:, g, first:last],
+                in_=a_grouped[:, first:last, :].rearrange("p c t -> p (c t)"),
+            )
 
         def c_pass(i, g):
             if g == 0:
@@ -311,31 +310,35 @@ def tile_mla_pb_kernel(tc, x, wkv_a, wkv_b, out_0, out_1):
             )
 
         def scale_c(i):
-            cn = stage.tile([P, PACK, P], BF16, name="cn")
+            cn = stage.tile([P, LATENT], BF16, name="cn")
             nc.scalar.activation(
                 out=cn[:],
-                in_=c_banks[i][:].rearrange("p (q t) -> p t q", t=PACK),
+                in_=c_banks[i][:],
                 func=ACT.Copy,
                 scale=inv_rms[:, i : i + 1],
             )
             return cn
 
         def transpose_cn(cn):
-            cn_bank = bank_tile([P, PACK, P], BF16)
-            for t in range(PACK):
-                nc.tensor.transpose(cn_bank[:, t, :], cn[:, t, :], ident_bf16[:])
+            words = cn[:].bitcast(F32).rearrange("p (q u) -> p u q", u=2)
+            cn_bank = bank_tile([P, 2, P], F32)
+            for u in range(2):
+                nc.tensor.transpose(cn_bank[:, u, :], words[:, u, :], ident_f32[:])
             return cn_bank
 
         def empty_cn(cn_bank, copy):
-            cn_grouped = stage.tile([P, P, PACK], BF16, name="cn_grouped", align_bytes=64)
-            copy(out=cn_grouped[:], in_=cn_bank[:].rearrange("p t w -> p w t"))
+            cn_grouped = stage.tile([P, P * PACK], BF16, name="cn_grouped", align_bytes=64)
+            copy(
+                out=cn_grouped[:].bitcast(F32).rearrange("p (w u) -> p w u", u=2),
+                in_=cn_bank[:].rearrange("p u w -> p w u"),
+            )
             return cn_grouped
 
         def quantise_cn(i, cn_grouped):
             nc.vector.quantize_mx(
                 out=cn_codes[:, i, :].bitcast(FP8X4),
                 scales=cn_scales[:, i, :],
-                in_=cn_grouped[:].rearrange("p w t -> p (w t)"),
+                in_=cn_grouped[:],
             )
 
         def empty_r(tiles, r_bank, copy):
@@ -362,14 +365,20 @@ def tile_mla_pb_kernel(tc, x, wkv_a, wkv_b, out_0, out_1):
                 .to_broadcast([P, CHUNK_HEADS, ROPE_DIM]),
             )
 
-        def regroup_b(kind, chunk):
+        def regroup_heads(kind, chunk, b_grouped, first, last):
+            by_head = b_grouped[:].rearrange("p (h c i) t -> p h c t i", h=CHUNK_HEADS, i=RUN)
+            raw = b_raw[chunk][:, :, :, kind, :].rearrange("p t h (c i) -> p h c t i", i=RUN)
+            nc.vector.tensor_copy(out=by_head[:, first:last], in_=raw[:, first:last])
+
+        def group_tile():
             b_grouped = b_stage.tile(
                 [P, CHUNK_HEADS * HEAD_DIM, PACK], BF16, name="b_grouped", align_bytes=64
             )
-            nc.vector.tensor_copy(
-                out=b_grouped[:].rearrange("p (h c i) t -> p h c t i", h=CHUNK_HEADS, i=RUN),
-                in_=b_raw[chunk][:, :, :, kind, :].rearrange("p t h (c i) -> p h c t i", i=RUN),
-            )
+            return b_grouped
+
+        def regroup_b(kind, chunk):
+            b_grouped = group_tile()
+            regroup_heads(kind, chunk, b_grouped, 0, CHUNK_HEADS)
             return b_grouped
 
         def quantise_b(kind, chunk, b_grouped):
@@ -393,6 +402,10 @@ def tile_mla_pb_kernel(tc, x, wkv_a, wkv_b, out_0, out_1):
                     stop=True,
                 )
             return u_bank
+
+        def finish_k(chunk, i, u_bank, copy):
+            empty_k(chunk, i, u_bank, copy)
+            store_k(chunk, 1, i)
 
         def empty_k(chunk, i, u_bank, copy):
             copy(out=k_out[i][:, chunk % K_SLOTS, :, 0:HEAD_DIM], in_=u_bank[:])
@@ -420,14 +433,16 @@ def tile_mla_pb_kernel(tc, x, wkv_a, wkv_b, out_0, out_1):
         ag0 = regroup_a(0)
         x0 = transpose_x(0)
         xg0 = empty_x(x0, (A, A))
-        quantise_a(0, ag0)
+        quantise_a(0, ag0, 0, LATENT)
+        quantise_a(0, ag0, LATENT, A_COLS)
         ag1 = regroup_a(1)
         quantise_x(0, xg0)
         warm_tensor(3)
         x1 = transpose_x(1)
         c_pass(0, 0)
         xg1 = empty_x(x1, (A, A))
-        quantise_a(1, ag1)
+        quantise_a(1, ag1, 0, LATENT)
+        quantise_a(1, ag1, LATENT, A_COLS)
         c_pass(0, 1)
         warm_tensor(2)
         ag2 = regroup_a(2)
@@ -436,113 +451,122 @@ def tile_mla_pb_kernel(tc, x, wkv_a, wkv_b, out_0, out_1):
         c_pass(1, 1)
         ag3 = regroup_a(3)
         x2 = transpose_x(2)
-        quantise_a(2, ag2)
+        quantise_a(2, ag2, 0, LATENT)
         c_pass(0, 2)
-        xg2 = empty_x(x2, (A, A))
-        quantise_a(3, ag3)
+        quantise_a(3, ag3, 0, LATENT)
         c_pass(0, 3)
+        xg2 = empty_x(x2, (A, A))
         c_pass(1, 2)
         c_pass(1, 3)
-        quantise_x(2, xg2)
+        quantise_a(2, ag2, LATENT, A_COLS)
+        quantise_a(3, ag3, LATENT, A_COLS)
+        bg = regroup_b(NOPE, 0)
         tiles = range(0, 2)
         r_bank = multiply_r(tiles)
         square_c(0)
-        bg = regroup_b(NOPE, 0)
-        for g in range(A_PASSES):
-            c_pass(2, g)
         square_c(1)
+        norm_factors(slice(0, 1))
         rt = empty_r(tiles, r_bank, A)
-        norm_factors(first)
+        quantise_x(2, xg2)
+        quantise_b(NOPE, 0, bg)
         rope_bank = rotate_rope_key(tiles, rt)
         cn0 = scale_c(0)
         t0 = transpose_cn(cn0)
-        quantise_b(NOPE, 0, bg)
+        norm_factors(slice(1, 2))
+        empty_rope_key(tiles, rope_bank, A)
+        bg = group_tile()
+        regroup_heads(NOPE, 1, bg, 0, 2)
         cn1 = scale_c(1)
         cg0 = empty_cn(t0, V)
+        for g in range(A_PASSES):
+            c_pass(2, g)
         t1 = transpose_cn(cn1)
-        empty_rope_key(tiles, rope_bank, A)
-        cg1 = empty_cn(t1, V)
         square_c(2)
-        tiles = range(2, 3)
-        r_bank = multiply_r(tiles)
-        quantise_cn(0, cg0)
-        rt = empty_r(tiles, r_bank, A)
-        quantise_cn(1, cg1)
-        u0 = multiply_b(NOPE, 0, 0, "c")
-        u1 = multiply_b(NOPE, 0, 1, "c")
         repeat_rope_key(0, 0)
-        rope_bank = rotate_rope_key(tiles, rt)
-        x3 = transpose_x(3)
-        bg = regroup_b(NOPE, 1)
+        quantise_cn(0, cg0)
+        regroup_heads(NOPE, 1, bg, 2, 4)
+        u0 = multiply_b(NOPE, 0, 0, "c")
+        cg1 = empty_cn(t1, V)
+        finish_k(0, 0, u0, A)
         norm_factors(slice(2, 3))
-        empty_k(0, 0, u0, A)
-        store_k(0, 1, 0)
-        cn2 = scale_c(2)
         repeat_rope_key(1, 0)
-        empty_k(0, 1, u1, A)
-        store_k(0, 1, 1)
-        t2 = transpose_cn(cn2)
-        empty_rope_key(tiles, rope_bank, A)
-        xg3 = empty_x(x3, (A, A))
+        quantise_cn(1, cg1)
+        cn2 = scale_c(2)
+        u1 = multiply_b(NOPE, 0, 1, "c")
         quantise_b(NOPE, 1, bg)
-        cg2 = empty_cn(t2, V)
+        finish_k(0, 1, u1, A)
+        tiles = range(2, 3)
+        t2 = transpose_cn(cn2)
+        r_bank = multiply_r(tiles)
         u0 = multiply_b(NOPE, 1, 0, "c")
         repeat_rope_key(0, 1)
-        u1 = multiply_b(NOPE, 1, 1, "c")
+        cg2 = empty_cn(t2, V)
+        rt = empty_r(tiles, r_bank, A)
+        finish_k(1, 0, u0, A)
+        u1 = multiply_b(NOPE, 1, 1)
+        rope_bank = rotate_rope_key(tiles, rt)
+        repeat_rope_key(1, 1)
         quantise_cn(2, cg2)
+        finish_k(1, 1, u1, A)
+        u0 = multiply_b(NOPE, 0, 2)
+        x3 = transpose_x(3)
+        empty_rope_key(tiles, rope_bank, A)
+        bg = regroup_b(NOPE, 2)
+        repeat_rope_key(2, 0)
+        finish_k(0, 2, u0, A)
+        u1 = multiply_b(NOPE, 1, 2)
+        xg3 = empty_x(x3, (A, A))
+        quantise_b(NOPE, 2, bg)
+        repeat_rope_key(2, 1)
+        finish_k(1, 2, u1, A)
+        u0 = multiply_b(NOPE, 2, 0, "c")
+        u1 = multiply_b(NOPE, 2, 1, "c")
         quantise_x(3, xg3)
-        u2 = multiply_b(NOPE, 0, 2)
-        u4 = multiply_b(NOPE, 1, 2)
         for g in range(A_PASSES):
             c_pass(3, g)
         tiles = range(3, 4)
         r_bank = multiply_r(tiles)
-        empty_k(1, 0, u0, A)
-        store_k(1, 1, 0)
-        repeat_rope_key(1, 1)
-        empty_k(1, 1, u1, A)
-        store_k(1, 1, 1)
-        repeat_rope_key(2, 0)
-        empty_k(0, 2, u2, A)
-        store_k(0, 1, 2)
-        repeat_rope_key(2, 1)
-        empty_k(1, 2, u4, A)
-        store_k(1, 1, 2)
+        bg = regroup_b(NOPE, 3)
+        finish_k(2, 0, u0, A)
+        finish_k(2, 1, u1, A)
+        u0 = multiply_b(NOPE, 2, 2)
         square_c(3)
         rt = empty_r(tiles, r_bank, A)
+        finish_k(2, 2, u0, A)
         norm_factors(slice(3, 4))
-        bg = regroup_b(NOPE, 2)
-        cn3 = scale_c(3)
         rope_bank = rotate_rope_key(tiles, rt)
+        quantise_b(NOPE, 3, bg)
+        u0 = multiply_b(NOPE, 3, 0)
+        cn3 = scale_c(3)
+        finish_k(3, 0, u0, A)
         t3 = transpose_cn(cn3)
         empty_rope_key(tiles, rope_bank, A)
-        quantise_b(NOPE, 2, bg)
-        for i in range(PAIR):
-            u = multiply_b(NOPE, 2, i, "c")
-            empty_k(2, i, u, A)
-            store_k(2, 1, i)
+        bg = regroup_b(VALUE, 0)
         cg3 = empty_cn(t3, V)
+        u1 = multiply_b(NOPE, 3, 1, "c")
         repeat_rope_key(3, 0)
         quantise_cn(3, cg3)
-        bg = regroup_b(NOPE, 3)
-        u3 = multiply_b(NOPE, 0, 3)
-        empty_k(0, 3, u3, A)
-        store_k(0, 1, 3)
-        u3 = multiply_b(NOPE, 1, 3, "c")
+        u0 = multiply_b(NOPE, 3, 2)
+        finish_k(3, 1, u1, A)
         repeat_rope_key(3, 1)
-        empty_k(1, 3, u3, A)
-        store_k(1, 1, 3)
-        quantise_b(NOPE, 3, bg)
+        bh = regroup_b(VALUE, 1)
+        quantise_b(VALUE, 0, bg)
+        u1 = multiply_b(NOPE, 0, 3, "c")
+        finish_k(3, 2, u0, A)
+        quantise_b(VALUE, 1, bh)
+        u0 = multiply_b(NOPE, 1, 3)
+        finish_k(0, 3, u1, A)
+        finish_k(1, 3, u0, A)
+        bg = regroup_b(VALUE, 2)
+        bh = regroup_b(VALUE, 3)
+        quantise_b(VALUE, 2, bg)
+        quantise_b(VALUE, 3, bh)
+        for i in range(PAIR):
+            multiply_and_store_v(0, 2, i, (A, A))
+        for chunk in range(2, 4):
+            u0 = multiply_b(NOPE, chunk, 3, ("any", "c")[chunk % 2])
+            finish_k(chunk, 3, u0, A)
+        for i in range(PAIR, TOKEN_TILES):
+            multiply_and_store_v(0, 2, i, (A, A))
         for i in range(TOKEN_TILES):
-            rest = range(3, 4) if i < PAIR else range(2, 4)
-            for chunk in rest:
-                u = multiply_b(NOPE, chunk, i, ("any", "c")[chunk - 2])
-                empty_k(chunk, i, u, A)
-            store_k(rest.start, len(rest), i)
-        for chunk in (0, 2):
-            bg = regroup_b(VALUE, chunk)
-            bh = regroup_b(VALUE, chunk + 1)
-            quantise_b(VALUE, chunk, bg)
-            quantise_b(VALUE, chunk + 1, bh)
-        for i in range(TOKEN_TILES):
-            multiply_and_store_v(0, CHUNKS, i, (A, V))
+            multiply_and_store_v(2, 2, i, (A, V))

import math
from contextlib import ExitStack

import concourse.mybir as mybir
from concourse.masks import make_identity

F32 = mybir.dt.float32
BF16 = mybir.dt.bfloat16
I32 = mybir.dt.int32
U32 = mybir.dt.uint32
U8 = mybir.dt.uint8
FP8X4 = mybir.dt.float8_e4m3fn_x4
ALU = mybir.AluOpType
ACT = mybir.ActivationFunctionType

P = 128
PACK = 4
K_PASS = P * PACK

TOKENS = 512
TOKEN_TILES = TOKENS // P
DIM = 2048
A_PASSES = DIM // K_PASS
LATENT = 512
ROPE_DIM = 128
HALF = ROPE_DIM // 2
A_COLS = LATENT + ROPE_DIM
HEADS = 16
HEAD_DIM = 128
EPS = 1e-6
ROPE_BASE = 10000.0
POSITION = 37

CHUNK_HEADS = 4
CHUNKS = HEADS // CHUNK_HEADS
CHUNK_COLS = CHUNK_HEADS * 2 * HEAD_DIM
NOPE = 0
VALUE = 1
A_VECTOR_COLS = 400
A_VECTOR_COLS_FIRST = 512
COARSE = 8
FINE = HALF // COARSE
RUN = 4
PSUM_BANKS = 8
V_BUFS = 8
K_SLOTS = 2
PAIR = 2

FLOPS = 2 * TOKENS * DIM * A_COLS + 2 * TOKENS * LATENT * HEADS * 2 * HEAD_DIM


def regroup(copy, grouped, raw):
    copy(
        out=grouped.rearrange("p (c i) t -> p c t i", i=RUN),
        in_=raw.rearrange("p t (c i) -> p c t i", i=RUN),
    )


def build_rotation(nc, pool, ident):
    powers = pool.tile([P, COARSE + FINE], F32, name="powers")
    one = pool.tile([P, 1], F32, name="one")
    nc.vector.memset(one[:], 1.0)
    exponents = [FINE * a for a in range(COARSE)] + list(range(FINE))
    for n, exponent in enumerate(exponents):
        nc.vector.tensor_scalar(
            out=powers[:, n : n + 1],
            in0=one[:],
            scalar1=ROPE_BASE ** (-exponent / HALF),
            scalar2=None,
            op0=ALU.mult,
        )
    shift = pool.tile([P, 2, HALF], F32, name="shift")
    per_turn = POSITION / (2.0 * math.pi)
    for f, quarter in enumerate((0.25, 0.0)):
        whole = [round(per_turn * ROPE_BASE ** (-j / HALF) + quarter) for j in range(HALF)]
        for number in sorted(set(whole)):
            begin = whole.index(number)
            end = begin + whole.count(number)
            nc.gpsimd.memset(shift[:, f, begin:end], quarter - number)
    theta = pool.tile([P, COARSE, FINE], F32, name="theta")
    nc.vector.tensor_tensor(
        out=theta[:],
        in0=powers[:, 0:COARSE].unsqueeze(2).to_broadcast([P, COARSE, FINE]),
        in1=powers[:, COARSE : COARSE + FINE].unsqueeze(1).to_broadcast([P, COARSE, FINE]),
        op=ALU.mult,
    )
    turns = pool.tile([P, 2, HALF], F32, name="turns")
    for f in range(2):
        nc.vector.scalar_tensor_tensor(
            out=turns[:, f, :],
            in0=theta[:].rearrange("p a b -> p (a b)"),
            scalar=per_turn,
            in1=shift[:, f, :],
            op0=ALU.mult,
            op1=ALU.add,
        )
    trig = pool.tile([P, 2, HALF], F32, name="trig")
    nc.scalar.activation(out=trig[:], in_=turns[:], func=ACT.Sin, scale=2.0 * math.pi)
    by_half = ident[:].rearrange("p (h j) -> p h j", h=2)
    cosines = pool.tile([P, 2, HALF], F32, name="cosines")
    nc.vector.tensor_tensor(
        out=cosines[:],
        in0=by_half,
        in1=trig[:, 0, :].unsqueeze(1).to_broadcast([P, 2, HALF]),
        op=ALU.mult,
    )
    sines = pool.tile([P, 2, HALF], F32, name="sines")
    for h in range(2):
        nc.vector.tensor_tensor(
            out=sines[:, h, :], in0=by_half[:, 1 - h, :], in1=trig[:, 1, :], op=ALU.mult
        )
    rotation = pool.tile([P, ROPE_DIM], F32, name="rotation")
    for h, op in enumerate((ALU.subtract, ALU.add)):
        nc.vector.tensor_tensor(
            out=rotation[:, h * HALF : (h + 1) * HALF],
            in0=cosines[:, h, :],
            in1=sines[:, h, :],
            op=op,
        )
    return rotation


def tile_mla_pb_kernel(tc, x, wkv_a, wkv_b, out_0, out_1):
    nc = tc.nc
    x_rows = x.rearrange("b s d -> (b s) d")
    k_rows = out_0.rearrange("b s h d -> (b s) h d")
    v_rows = out_1.rearrange("b s h d -> (b s) h d")

    with ExitStack() as stack:
        stack.enter_context(tc.manual_schedule())
        keep = stack.enter_context(tc.tile_pool(name="keep", bufs=1))
        stage = stack.enter_context(tc.tile_pool(name="stage", bufs=2))
        b_stage = stack.enter_context(tc.tile_pool(name="b_stage", bufs=2))
        outs = stack.enter_context(tc.tile_pool(name="outs", bufs=V_BUFS))
        psum = stack.enter_context(tc.psum_pool(name="psum", bufs=PSUM_BANKS // 2))

        x_raw = [None] * TOKEN_TILES
        a_raw = [None] * A_PASSES
        b_raw = [None] * CHUNKS

        def load_x(i):
            raw = keep.tile([P, DIM], BF16, name="x_raw%d" % i)
            nc.sync.dma_start(out=raw[:], in_=x_rows[i * P : (i + 1) * P, :])
            x_raw[i] = raw

        def load_a(g):
            raw = keep.tile([P, PACK, A_COLS], BF16, name="a_raw%d" % g)
            rows = wkv_a[g * K_PASS : (g + 1) * K_PASS, :]
            nc.sync.dma_start(out=raw[:], in_=rows.rearrange("(p t) c -> p t c", t=PACK))
            a_raw[g] = raw

        def load_b(first, count):
            raw = keep.tile(
                [P, PACK, count * CHUNK_HEADS, 2, HEAD_DIM], BF16, name="b_raw%d" % first
            )
            cols = wkv_b[:, first * CHUNK_COLS : (first + count) * CHUNK_COLS]
            nc.sync.dma_start(
                out=raw[:].rearrange("p t h f d -> p t (h f d)"),
                in_=cols.rearrange("(p t) c -> p t c", t=PACK),
            )
            for n in range(count):
                b_raw[first + n] = raw[:, :, n * CHUNK_HEADS : (n + 1) * CHUNK_HEADS, :, :]

        load_a(0)
        load_x(0)
        load_a(1)
        load_x(1)
        load_a(2)
        load_a(3)
        load_x(2)
        load_b(0, 1)
        load_b(1, 1)
        load_x(3)
        load_b(2, 2)

        ident_f32 = keep.tile([P, P], F32, name="ident_f32")
        make_identity(nc, ident_f32[:])
        ident_bf16 = keep.tile([P, P], BF16, name="ident_bf16")
        make_identity(nc, ident_bf16[:])
        zeros = keep.tile([P, LATENT], BF16, name="zeros")
        nc.vector.memset(zeros[:], 0.0)
        eps = keep.tile([P, 1], F32, name="eps")
        nc.vector.memset(eps[:], EPS)
        warm_up = keep.tile([P, 2], F32, name="warm_up")
        nc.scalar.activation(out=warm_up[:, 0:1], in_=eps[:], func=ACT.Sin)
        rotation = build_rotation(nc, keep, ident_f32)
        nc.scalar.activation(out=warm_up[:, 1:2], in_=eps[:], func=ACT.Abs_reciprocal_sqrt)

        def warm_tensor(count):
            idle_bank = psum.tile([P, LATENT], F32, name="any_bank")
            for n in range(count):
                nc.tensor.matmul(
                    idle_bank[:], lhsT=zeros[:, 0:P], rhs=zeros[:], start=True, stop=True
                )

        x_codes = keep.tile([P, TOKEN_TILES, A_PASSES, P], U32, name="x_codes", align_bytes=64)
        x_scales = keep.tile([P, TOKEN_TILES, A_PASSES, P], U8, name="x_scales", align_bytes=64)
        a_codes = keep.tile([P, A_PASSES, A_COLS], U32, name="a_codes", align_bytes=64)
        a_scales = keep.tile([P, A_PASSES, A_COLS], U8, name="a_scales", align_bytes=64)
        cn_codes = keep.tile([P, TOKEN_TILES, P], U32, name="cn_codes", align_bytes=64)
        cn_scales = keep.tile([P, TOKEN_TILES, P], U8, name="cn_scales", align_bytes=64)
        b_codes = keep.tile([P, 2, HEADS, HEAD_DIM], U32, name="b_codes", align_bytes=64)
        b_scales = keep.tile([P, 2, HEADS, HEAD_DIM], U8, name="b_scales", align_bytes=64)

        def bank_tile(shape, dtype, kind="any"):
            bank = psum.tile(shape, dtype, name=kind + "_bank")
            return bank

        sum_squares = keep.tile([P, TOKEN_TILES], F32, name="sum_squares")
        inv_rms = keep.tile([P, TOKEN_TILES], F32, name="inv_rms")
        rope = keep.tile([P, TOKEN_TILES, ROPE_DIM], F32, name="rope")
        k_out = []
        for i in range(TOKEN_TILES):
            k_tile = keep.tile(
                [P, K_SLOTS, CHUNK_HEADS, HEAD_DIM + ROPE_DIM], F32, name="k_out%d" % i
            )
            k_out.append(k_tile)
        c_banks = {}

        def transpose_x(i):
            words = x_raw[i][:].bitcast(F32).rearrange("p (g q u) -> p g u q", g=A_PASSES, u=2)
            banks = []
            for half in range(2):
                x_bank = bank_tile([P, 2, 2, P], F32)
                for g in range(2):
                    for u in range(2):
                        nc.tensor.transpose(
                            x_bank[:, g, u, :], words[:, 2 * half + g, u, :], ident_f32[:]
                        )
                banks.append(x_bank)
            return banks

        def empty_x(banks, copies):
            x_grouped = stage.tile([P, A_PASSES * P * PACK], BF16, name="x_grouped", align_bytes=64)
            grouped_words = x_grouped[:].bitcast(F32).rearrange(
                "p (g w u) -> p g w u", g=A_PASSES, u=2
            )
            for half, (x_bank, copy) in enumerate(zip(banks, copies)):
                copy(
                    out=grouped_words[:, 2 * half : 2 * half + 2, :, :],
                    in_=x_bank[:].rearrange("p g u w -> p g w u"),
                )
            return x_grouped

        def quantise_x(i, x_grouped):
            nc.vector.quantize_mx(
                out=x_codes[:, i, :, :].rearrange("p g w -> p (g w)").bitcast(FP8X4),
                scales=x_scales[:, i, :, :].rearrange("p g w -> p (g w)"),
                in_=x_grouped[:],
            )

        def regroup_a(g):
            a_grouped = stage.tile([P, A_COLS, PACK], BF16, name="a_grouped", align_bytes=64)
            split = A_VECTOR_COLS_FIRST if g == 0 else A_VECTOR_COLS
            regroup(nc.vector.tensor_copy, a_grouped[:, 0:split, :], a_raw[g][:, :, 0:split])
            regroup(nc.scalar.copy, a_grouped[:, split:A_COLS, :], a_raw[g][:, :, split:A_COLS])
            return a_grouped

        def quantise_a(g, a_grouped, first, last):
            nc.vector.quantize_mx(
                out=a_codes[:, g, first:last].bitcast(FP8X4),
                scales=a_scales[:, g, first:last],
                in_=a_grouped[:, first:last, :].rearrange("p c t -> p (c t)"),
            )

        def c_pass(i, g):
            if g == 0:
                c_banks[i] = bank_tile([P, LATENT], F32, "c")
            nc.tensor.matmul_mx(
                out=c_banks[i][:],
                lhsT=x_codes[:, i, g, :].bitcast(FP8X4),
                lhsT_scale=x_scales[:, i, g, :],
                rhs=a_codes[:, g, 0:LATENT].bitcast(FP8X4),
                rhs_scale=a_scales[:, g, 0:LATENT],
                start=(g == 0),
                stop=(g == A_PASSES - 1),
            )

        def multiply_r(tiles):
            r_bank = bank_tile([P, len(tiles), P], F32)
            for n, i in enumerate(tiles):
                for g in range(A_PASSES):
                    nc.tensor.matmul_mx(
                        out=r_bank[:, n, :],
                        lhsT=a_codes[:, g, LATENT:A_COLS].bitcast(FP8X4),
                        lhsT_scale=a_scales[:, g, LATENT:A_COLS],
                        rhs=x_codes[:, i, g, :].bitcast(FP8X4),
                        rhs_scale=x_scales[:, i, g, :],
                        start=(g == 0),
                        stop=(g == A_PASSES - 1),
                    )
            return r_bank

        def square_c(i):
            squares = stage.tile([P, LATENT], F32, name="squares")
            nc.scalar.activation(
                out=squares[:],
                in_=c_banks[i][:],
                func=ACT.Square,
                accum_out=sum_squares[:, i : i + 1],
            )

        def norm_factors(tiles):
            nc.scalar.activation(
                out=inv_rms[:, tiles],
                in_=sum_squares[:, tiles],
                func=ACT.Abs_reciprocal_sqrt,
                scale=1.0 / LATENT,
                bias=eps[:],
            )

        def scale_c(i):
            cn = stage.tile([P, LATENT], BF16, name="cn")
            nc.scalar.activation(
                out=cn[:],
                in_=c_banks[i][:],
                func=ACT.Copy,
                scale=inv_rms[:, i : i + 1],
            )
            return cn

        def transpose_cn(cn):
            words = cn[:].bitcast(F32).rearrange("p (q u) -> p u q", u=2)
            cn_bank = bank_tile([P, 2, P], F32)
            for u in range(2):
                nc.tensor.transpose(cn_bank[:, u, :], words[:, u, :], ident_f32[:])
            return cn_bank

        def empty_cn(cn_bank, copy):
            cn_grouped = stage.tile([P, P * PACK], BF16, name="cn_grouped", align_bytes=64)
            copy(
                out=cn_grouped[:].bitcast(F32).rearrange("p (w u) -> p w u", u=2),
                in_=cn_bank[:].rearrange("p u w -> p w u"),
            )
            return cn_grouped

        def quantise_cn(i, cn_grouped):
            nc.vector.quantize_mx(
                out=cn_codes[:, i, :].bitcast(FP8X4),
                scales=cn_scales[:, i, :],
                in_=cn_grouped[:],
            )

        def empty_r(tiles, r_bank, copy):
            r_transposed = stage.tile([P, len(tiles), P], F32, name="r_transposed")
            copy(out=r_transposed[:], in_=r_bank[:])
            return r_transposed

        def rotate_rope_key(tiles, r_transposed):
            rope_bank = bank_tile([P, len(tiles), ROPE_DIM], F32)
            for n in range(len(tiles)):
                nc.tensor.matmul(
                    rope_bank[:, n, :], lhsT=r_transposed[:, n, :], rhs=rotation[:], start=True, stop=True
                )
            return rope_bank

        def empty_rope_key(tiles, rope_bank, copy):
            copy(out=rope[:, tiles.start : tiles.stop, :], in_=rope_bank[:])

        def repeat_rope_key(i, slot):
            nc.vector.tensor_copy(
                out=k_out[i][:, slot, :, HEAD_DIM : HEAD_DIM + ROPE_DIM],
                in_=rope[:, i, :]
                .unsqueeze(1)
                .to_broadcast([P, CHUNK_HEADS, ROPE_DIM]),
            )

        def regroup_heads(kind, chunk, b_grouped, first, last):
            by_head = b_grouped[:].rearrange("p (h c i) t -> p h c t i", h=CHUNK_HEADS, i=RUN)
            raw = b_raw[chunk][:, :, :, kind, :].rearrange("p t h (c i) -> p h c t i", i=RUN)
            nc.vector.tensor_copy(out=by_head[:, first:last], in_=raw[:, first:last])

        def group_tile():
            b_grouped = b_stage.tile(
                [P, CHUNK_HEADS * HEAD_DIM, PACK], BF16, name="b_grouped", align_bytes=64
            )
            return b_grouped

        def regroup_b(kind, chunk):
            b_grouped = group_tile()
            regroup_heads(kind, chunk, b_grouped, 0, CHUNK_HEADS)
            return b_grouped

        def quantise_b(kind, chunk, b_grouped):
            heads = slice(chunk * CHUNK_HEADS, (chunk + 1) * CHUNK_HEADS)
            nc.vector.quantize_mx(
                out=b_codes[:, kind, heads, :].rearrange("p h d -> p (h d)").bitcast(FP8X4),
                scales=b_scales[:, kind, heads, :].rearrange("p h d -> p (h d)"),
                in_=b_grouped[:].rearrange("p c t -> p (c t)"),
            )

        def multiply_b(kind, chunk, i, bank="any"):
            u_bank = bank_tile([P, CHUNK_HEADS, HEAD_DIM], F32, bank)
            for h in range(CHUNK_HEADS):
                nc.tensor.matmul_mx(
                    out=u_bank[:, h, :],
                    lhsT=cn_codes[:, i, :].bitcast(FP8X4),
                    lhsT_scale=cn_scales[:, i, :],
                    rhs=b_codes[:, kind, chunk * CHUNK_HEADS + h, :].bitcast(FP8X4),
                    rhs_scale=b_scales[:, kind, chunk * CHUNK_HEADS + h, :],
                    start=True,
                    stop=True,
                )
            return u_bank

        def finish_k(chunk, i, u_bank, copy):
            empty_k(chunk, i, u_bank, copy)
            store_k(chunk, 1, i)

        def empty_k(chunk, i, u_bank, copy):
            copy(out=k_out[i][:, chunk % K_SLOTS, :, 0:HEAD_DIM], in_=u_bank[:])

        def store_k(first, count, i):
            slot = first % K_SLOTS
            nc.sync.dma_start(
                out=k_rows[i * P : (i + 1) * P, first * CHUNK_HEADS : (first + count) * CHUNK_HEADS, :],
                in_=k_out[i][:, slot : slot + count, :, :].rearrange("p s h d -> p (s h) d"),
            )

        def multiply_and_store_v(first, count, i, copies):
            v_out = outs.tile([P, count, CHUNK_HEADS, HEAD_DIM], F32, name="v_out")
            for n in range(count):
                u_bank = multiply_b(VALUE, first + n, i, ("any", "c")[n % 2])
                copies[n % 2](out=v_out[:, n, :, :], in_=u_bank[:])
            nc.sync.dma_start(
                out=v_rows[i * P : (i + 1) * P, first * CHUNK_HEADS : (first + count) * CHUNK_HEADS, :],
                in_=v_out[:].rearrange("p s h d -> p (s h) d"),
            )

        V, A = nc.vector.tensor_copy, nc.scalar.copy
        first, second = slice(0, PAIR), slice(PAIR, 2 * PAIR)
        warm_tensor(10)
        ag0 = regroup_a(0)
        x0 = transpose_x(0)
        xg0 = empty_x(x0, (A, A))
        quantise_a(0, ag0, 0, LATENT)
        quantise_a(0, ag0, LATENT, A_COLS)
        ag1 = regroup_a(1)
        quantise_x(0, xg0)
        warm_tensor(3)
        x1 = transpose_x(1)
        c_pass(0, 0)
        xg1 = empty_x(x1, (A, A))
        quantise_a(1, ag1, 0, LATENT)
        quantise_a(1, ag1, LATENT, A_COLS)
        c_pass(0, 1)
        warm_tensor(2)
        ag2 = regroup_a(2)
        quantise_x(1, xg1)
        c_pass(1, 0)
        c_pass(1, 1)
        ag3 = regroup_a(3)
        x2 = transpose_x(2)
        quantise_a(2, ag2, 0, LATENT)
        c_pass(0, 2)
        quantise_a(3, ag3, 0, LATENT)
        c_pass(0, 3)
        xg2 = empty_x(x2, (A, A))
        c_pass(1, 2)
        c_pass(1, 3)
        quantise_a(2, ag2, LATENT, A_COLS)
        quantise_a(3, ag3, LATENT, A_COLS)
        bg = regroup_b(NOPE, 0)
        tiles = range(0, 2)
        r_bank = multiply_r(tiles)
        square_c(0)
        square_c(1)
        norm_factors(slice(0, 1))
        rt = empty_r(tiles, r_bank, A)
        quantise_x(2, xg2)
        quantise_b(NOPE, 0, bg)
        rope_bank = rotate_rope_key(tiles, rt)
        cn0 = scale_c(0)
        t0 = transpose_cn(cn0)
        norm_factors(slice(1, 2))
        empty_rope_key(tiles, rope_bank, A)
        bg = group_tile()
        regroup_heads(NOPE, 1, bg, 0, 2)
        cn1 = scale_c(1)
        cg0 = empty_cn(t0, V)
        for g in range(A_PASSES):
            c_pass(2, g)
        t1 = transpose_cn(cn1)
        square_c(2)
        repeat_rope_key(0, 0)
        quantise_cn(0, cg0)
        regroup_heads(NOPE, 1, bg, 2, 4)
        u0 = multiply_b(NOPE, 0, 0, "c")
        cg1 = empty_cn(t1, V)
        finish_k(0, 0, u0, A)
        norm_factors(slice(2, 3))
        repeat_rope_key(1, 0)
        quantise_cn(1, cg1)
        cn2 = scale_c(2)
        u1 = multiply_b(NOPE, 0, 1, "c")
        quantise_b(NOPE, 1, bg)
        finish_k(0, 1, u1, A)
        tiles = range(2, 3)
        t2 = transpose_cn(cn2)
        r_bank = multiply_r(tiles)
        u0 = multiply_b(NOPE, 1, 0, "c")
        repeat_rope_key(0, 1)
        cg2 = empty_cn(t2, V)
        rt = empty_r(tiles, r_bank, A)
        finish_k(1, 0, u0, A)
        u1 = multiply_b(NOPE, 1, 1)
        rope_bank = rotate_rope_key(tiles, rt)
        repeat_rope_key(1, 1)
        quantise_cn(2, cg2)
        finish_k(1, 1, u1, A)
        u0 = multiply_b(NOPE, 0, 2)
        x3 = transpose_x(3)
        empty_rope_key(tiles, rope_bank, A)
        bg = regroup_b(NOPE, 2)
        repeat_rope_key(2, 0)
        finish_k(0, 2, u0, A)
        u1 = multiply_b(NOPE, 1, 2)
        xg3 = empty_x(x3, (A, A))
        quantise_b(NOPE, 2, bg)
        repeat_rope_key(2, 1)
        finish_k(1, 2, u1, A)
        u0 = multiply_b(NOPE, 2, 0, "c")
        u1 = multiply_b(NOPE, 2, 1, "c")
        quantise_x(3, xg3)
        for g in range(A_PASSES):
            c_pass(3, g)
        tiles = range(3, 4)
        r_bank = multiply_r(tiles)
        bg = regroup_b(NOPE, 3)
        finish_k(2, 0, u0, A)
        finish_k(2, 1, u1, A)
        u0 = multiply_b(NOPE, 2, 2)
        square_c(3)
        rt = empty_r(tiles, r_bank, A)
        finish_k(2, 2, u0, A)
        norm_factors(slice(3, 4))
        rope_bank = rotate_rope_key(tiles, rt)
        quantise_b(NOPE, 3, bg)
        u0 = multiply_b(NOPE, 3, 0)
        cn3 = scale_c(3)
        finish_k(3, 0, u0, A)
        t3 = transpose_cn(cn3)
        empty_rope_key(tiles, rope_bank, A)
        bg = regroup_b(VALUE, 0)
        cg3 = empty_cn(t3, V)
        u1 = multiply_b(NOPE, 3, 1, "c")
        repeat_rope_key(3, 0)
        quantise_cn(3, cg3)
        u0 = multiply_b(NOPE, 3, 2)
        finish_k(3, 1, u1, A)
        repeat_rope_key(3, 1)
        bh = regroup_b(VALUE, 1)
        quantise_b(VALUE, 0, bg)
        u1 = multiply_b(NOPE, 0, 3, "c")
        finish_k(3, 2, u0, A)
        quantise_b(VALUE, 1, bh)
        u0 = multiply_b(NOPE, 1, 3)
        finish_k(0, 3, u1, A)
        finish_k(1, 3, u0, A)
        bg = regroup_b(VALUE, 2)
        bh = regroup_b(VALUE, 3)
        quantise_b(VALUE, 2, bg)
        quantise_b(VALUE, 3, bh)
        for i in range(PAIR):
            multiply_and_store_v(0, 2, i, (A, A))
        for chunk in range(2, 4):
            u0 = multiply_b(NOPE, chunk, 3, ("any", "c")[chunk % 2])
            finish_k(chunk, 3, u0, A)
        for i in range(PAIR, TOKEN_TILES):
            multiply_and_store_v(0, 2, i, (A, A))
        for i in range(TOKEN_TILES):
            multiply_and_store_v(2, 2, i, (A, V))
